import numpy as np
import ml_dtypes


def mxq(x, axis, fmt="e4m3"):
    dtype, down = {"e4m3": (ml_dtypes.float8_e4m3fn, 7), "e5m2": (ml_dtypes.float8_e5m2, 14)}[fmt]
    v = np.moveaxis(np.asarray(x, np.float32).astype(ml_dtypes.bfloat16).astype(np.float64), axis, -1)
    blocks = v.reshape(v.shape[:-1] + (-1, 32))
    amax = np.abs(blocks).max(-1, keepdims=True)
    byte = np.maximum(np.where(amax > 0, np.frexp(amax)[1] - 1 + 127, 0) - down, 1)
    scale = np.exp2(byte - 127.0)
    codes = (blocks / scale).astype(np.float32).astype(dtype).astype(np.float64)
    return np.moveaxis((codes * scale).reshape(v.shape), -1, axis)


WIDE = False


def mx_kscale(k):
    if not WIDE:
        return np.ones(k)
    levels = np.array([10, -10, 5, -5, 0])
    a = np.random.permutation(np.resize(levels, k // 512 * 4)).reshape(k // 512, 4)
    idx = np.arange(k)
    return np.exp2(a[idx // 512, idx % 128 // 32])


BF16 = ml_dtypes.bfloat16


def bf(x):
    return np.asarray(x, np.float32).astype(BF16)


def f64(x):
    return np.asarray(x).astype(np.float64)


N, M, D, K = 1024, 1024, 512, 3
SLOPE = 0.01


def leaky_relu(v):
    return np.where(v >= 0.0, v, SLOPE * v)


def setup_inputs():
    s = mx_kscale(D)
    adj = np.random.uniform(size=(N, M)) ** 2 * (0.5 + np.random.uniform(size=(N, 1))) * (0.5 + np.random.uniform(size=(1, M)))
    return {"p_outgoing": bf(np.random.standard_normal((N, D)) * 0.1 * np.sqrt(N) * s),
            "q_incoming": bf(np.random.standard_normal((M, D)) * 0.1 * np.sqrt(M) * s),
            "adjacency_matrix": bf(adj),
            "Ws": bf(np.random.standard_normal((K, D, D)) * 2.0 / np.sqrt(D) / s),
            "bs": bf(np.random.standard_normal((K, D)) * 0.1 - 0.1)}


def reference(p_outgoing, q_incoming, adjacency_matrix, Ws, bs):
    A = f64(adjacency_matrix)
    d_out = A.sum(axis=0)
    d_in = A.sum(axis=1)
    wsq = mxq(f64(Ws).transpose(0, 2, 1), 1, "e4m3")
    Wp = (mxq(f64(p_outgoing), 1, "e4m3") @ wsq) + f64(bs)[:, None, :]
    Wq = (mxq(f64(q_incoming), 1, "e4m3") @ wsq) + f64(bs)[:, None, :]
    p_k = leaky_relu((mxq(A.T, 1, "e4m3") @ mxq(Wp, 1, "e4m3")) / d_out[None, :, None])
    q_k = leaky_relu((mxq(A, 1, "e4m3") @ mxq(Wq, 1, "e4m3")) / d_in[None, :, None])
    return p_k, q_k

@@ -1,0 +1,297 @@
+from contextlib import ExitStack
+
+import concourse.mybir as mybir
+from concourse.masks import make_identity
+
+FP8X4 = mybir.dt.float8_e4m3fn_x4
+BF16 = mybir.dt.bfloat16
+F32 = mybir.dt.float32
+U32 = mybir.dt.uint32
+U8 = mybir.dt.uint8
+ALU = mybir.AluOpType
+ACT = mybir.ActivationFunctionType
+AX = mybir.AxisListType
+
+P = 128
+NODES = 1024
+D = 512
+K = 3
+SLOPE = 0.01
+FLOPS = 2 * 2 * K * NODES * D * (D + NODES)
+
+UNITS = [(0, 0), (1, 0), (2, 0), (0, 1), (1, 1), (2, 1)]
+
+PROGRAM = [
+    ("TB", 0, 0, 0, 1), ("TB", 0, 0, 1, 0), ("TB", 1, 0, 0, 1), ("QWS", 0), ("TB", 1, 0, 1, 0), ("QNT", 0, 0),
+    ("TB", 1, 1, 0, 0), ("TB", 1, 1, 1, 1), ("QNT", 0, 1), ("S1", 0), ("S1", 1), ("RG", 0, 1, 0),
+    ("S1", 2), ("S1", 3), ("S1", 4), ("RG", 0, 0, 0), ("S1", 5), ("S1", 6),
+    ("S1", 7), ("QW", 0, 0), ("DIN", 0), ("QW", 0, 1), ("RG", 1, 0, 0), ("DOUT",),
+    ("RG", 1, 1, 0), ("QADJ", 0, 0, 1), ("QADJ", 0, 0, 0), ("QADJ", 0, 1, 0), ("QADJ", 0, 1, 1), ("TB", 0, 1, 1, 0),
+    ("TB", 0, 1, 0, 0), ("QWS", 1), ("TB", 0, 2, 1, 0), ("DIN", 1), ("TB", 0, 2, 0, 0), ("QWS", 2),
+    ("TB", 2, 1, 0, 0), ("S2", 0, 1), ("S1", 8), ("S1", 9), ("DINF",), ("S2", 1, 1),
+    ("S1", 10), ("S2", 2, 1), ("S1", 11), ("S1", 12), ("S1", 13), ("S1", 14),
+    ("S2", 3, 0), ("TB", 3, 1, 1, 0), ("S1", 15), ("QW", 1, 0), ("QW", 1, 1), ("S2", 4, 0),
+    ("S2", 5, 1), ("S2", 6, 1), ("S1", 16), ("S1", 17), ("S1", 18), ("S1", 19),
+    ("QW", 2, 0), ("TB", 2, 1, 1, 0), ("QNT", 1, 1), ("TB", 2, 0, 0, 0), ("TB", 2, 0, 1, 0), ("QNT", 1, 0),
+    ("S2", 7, 1), ("S2", 8, 0), ("S2", 9, 1), ("S1", 20), ("S1", 21), ("S1", 22),
+    ("S1", 23), ("QW", 2, 1), ("TB", 3, 0, 0, 0), ("TB", 3, 0, 2, 0), ("S2", 10, 1), ("S2", 11, 1),
+    ("S1", 24), ("S1", 25), ("S1", 26), ("S2", 12, 1), ("S1", 27), ("S1", 28),
+    ("S1", 29), ("S1", 30), ("S2", 13, 1), ("S1", 31), ("S2", 14, 0), ("S2", 15, 0),
+    ("S2", 16, 1), ("S1", 32), ("S1", 33), ("S1", 34), ("TB", 3, 0, 1, 0), ("QADJ", 1, 0, 0),
+    ("TB", 3, 1, 0, 0), ("QW", 3, 0), ("QADJ", 1, 1, 0), ("S2", 17, 0), ("S2", 18, 0), ("S2", 19, 1),
+    ("S2", 20, 1), ("S1", 35), ("S1", 36), ("S1", 37), ("TB", 3, 1, 2, 0), ("QW", 3, 1),
+    ("S1", 38), ("S2", 21, 0), ("TB", 3, 0, 3, 0), ("S2", 22, 1), ("S2", 23, 0), ("QADJ", 1, 0, 1),
+    ("TB", 3, 1, 3, 0), ("QADJ", 1, 1, 1), ("QW", 4, 0), ("S2", 24, 1), ("S2", 25, 0), ("S2", 26, 0),
+    ("S1", 39), ("S2", 27, 1), ("S1", 40), ("S1", 41), ("QW", 4, 1), ("S2", 28, 0),
+    ("S2", 29, 1), ("S1", 42), ("S1", 43), ("S2", 30, 0), ("S2", 31, 1), ("S2", 32, 0),
+    ("S2", 33, 1), ("S1", 44), ("S1", 45), ("S1", 46), ("S1", 47), ("S2", 34, 1),
+    ("S2", 35, 0), ("S2", 36, 0), ("QW", 5, 0), ("QW", 5, 1), ("S2", 37, 0), ("S2", 38, 0),
+    ("S2", 39, 1), ("S2", 40, 0), ("S2", 41, 0), ("S2", 42, 0), ("S2", 43, 0), ("S2", 44, 0),
+    ("S2", 45, 0), ("S2", 46, 0), ("S2", 47, 0),
+]
+
+
+def tile_gglr_pa_kernel(tc, p_outgoing, q_incoming, adjacency_matrix, Ws, bs, out_0, out_1):
+    nc = tc.nc
+    with ExitStack() as ctx:
+        keep = ctx.enter_context(tc.tile_pool(name="keep", bufs=1))
+        wpool = ctx.enter_context(tc.tile_pool(name="wpool", bufs=2))
+        work = ctx.enter_context(tc.tile_pool(name="work", bufs=4))
+        outp = ctx.enter_context(tc.tile_pool(name="outp", bufs=6))
+        psum = ctx.enter_context(tc.psum_pool(name="psum", bufs=8))
+        ctx.enter_context(tc.manual_schedule())
+
+        ident_f = keep.tile([P, P], F32)
+        make_identity(nc, ident_f[:])
+        ident_b = keep.tile([P, P], BF16)
+        make_identity(nc, ident_b[:])
+        ones = keep.tile([P, 32], BF16)
+        nc.vector.memset(ones[:], 1.0)
+        bias_sb = keep.tile([P, K * D], BF16)
+        nc.scalar.dma_start(out=bias_sb[:], in_=bs.rearrange("k d -> (k d)").partition_broadcast(P))
+
+        ws_nat = keep.tile([P, K, 4, D], BF16)
+        p_nat = keep.tile([P, 2, 4, D], BF16)
+        q_nat = keep.tile([P, 2, 4, D], BF16)
+        a_nat = keep.tile([P, 2, 4, NODES], BF16)
+
+        def load_ws(k, o0, o1):
+            nc.sync.dma_start(
+                out=ws_nat[:, k, o0:o1],
+                in_=Ws[k, o0 * P:o1 * P, :].rearrange("(o r) i -> r o i", r=P),
+            )
+
+        def load_p(c, t0, t1):
+            nc.sync.dma_start(
+                out=p_nat[:, c, t0:t1],
+                in_=p_outgoing[c * 512:(c + 1) * 512, :].rearrange("(p t) d -> p t d", t=4)[:, t0:t1, :],
+            )
+
+        def load_q(g):
+            nc.sync.dma_start(
+                out=q_nat[:, g].rearrange("p (u e) d -> p u e d", u=2),
+                in_=q_incoming[g * 512:(g + 1) * 512, :].rearrange("(u p e) d -> p u e d", u=2, e=2),
+            )
+
+        def load_a(c):
+            nc.sync.dma_start(
+                out=a_nat[:, c],
+                in_=adjacency_matrix[c * 512:(c + 1) * 512, :].rearrange("(p t) j -> p t j", t=4),
+            )
+
+        load_ws(0, 0, 2)
+        load_ws(0, 2, 4)
+        load_p(0, 0, 2)
+        load_p(0, 2, 4)
+        load_p(1, 0, 4)
+        load_a(0)
+        load_a(1)
+        load_ws(1, 0, 4)
+        load_ws(2, 0, 4)
+        load_q(0)
+        load_q(1)
+
+        wst_grp = keep.tile([P, K * D * 4], BF16, align_bytes=64)
+        wst_codes = keep.tile([P, K, D], U32, align_bytes=64)
+        wst_scales = keep.tile([P, K, D], U8, align_bytes=64)
+        nt_grp = [keep.tile([P, NODES * 4], BF16, align_bytes=64, name="nt_grp%d" % s) for s in range(2)]
+        nt_codes = [keep.tile([P, NODES], U32, align_bytes=64, name="nt_codes%d" % s) for s in range(2)]
+        nt_scales = [keep.tile([P, NODES], U8, align_bytes=64, name="nt_scales%d" % s) for s in range(2)]
+        adj_grp = [keep.tile([P, 2 * NODES * 4], BF16, align_bytes=64, name="adj_grp%d" % s) for s in range(2)]
+        adj_codes = [keep.tile([P, 2, NODES], U32, align_bytes=64, name="adj_codes%d" % s) for s in range(2)]
+        adj_scales = [keep.tile([P, 2, NODES], U8, align_bytes=64, name="adj_scales%d" % s) for s in range(2)]
+
+        def copy_on(eng, out, in_):
+            if eng == 0:
+                nc.scalar.copy(out=out, in_=in_)
+            else:
+                nc.vector.tensor_copy(out=out, in_=in_)
+
+        def tblock(words, grp, col0, eng):
+            tp = psum.tile([P, 2, 256], F32, tag="bank")
+            for h in range(2):
+                for u in range(2):
+                    nc.tensor.transpose(tp[:, u, h * P:(h + 1) * P], words[h][:, u * P:(u + 1) * P], ident_f[:])
+            dst = grp[:].bitcast(F32)[:, col0 * 2:(col0 + 256) * 2].rearrange("p (r u) -> p r u", u=2)
+            copy_on(eng, dst, tp[:].rearrange("p u r -> p r u"))
+
+        def op_tb(kind, a, b, eng):
+            if kind == 0:
+                tblock([ws_nat[:, a, 2 * b + i, :].bitcast(F32) for i in range(2)], wst_grp, a * D + b * 256, eng)
+            elif kind == 3:
+                words = []
+                for i in range(2):
+                    m = 2 * b + i
+                    words.append(a_nat[:, m // 4, m % 4, :].bitcast(F32)[:, a * 256:(a + 1) * 256])
+                tblock(words, adj_grp[1], a * NODES + b * 256, eng)
+            else:
+                nat = p_nat if kind == 1 else q_nat
+                tblock([nat[:, a, 2 * b + i, :].bitcast(F32) for i in range(2)], nt_grp[kind - 1], a * 512 + b * 256, eng)
+
+        def op_qws(k):
+            nc.vector.quantize_mx(
+                out=wst_codes[:, k, :].bitcast(FP8X4),
+                scales=wst_scales[:, k, :],
+                in_=wst_grp[:, k * D * 4:(k + 1) * D * 4],
+            )
+
+        def op_qnt(side, c):
+            nc.vector.quantize_mx(
+                out=nt_codes[side][:, c * 512:(c + 1) * 512].bitcast(FP8X4),
+                scales=nt_scales[side][:, c * 512:(c + 1) * 512],
+                in_=nt_grp[side][:, c * 2048:(c + 1) * 2048],
+            )
+
+        def op_rg(c, half, eng):
+            j0 = half * 512
+            dst = adj_grp[0][:, (c * NODES + j0) * 4:(c * NODES + j0 + 512) * 4]
+            copy_on(
+                eng,
+                dst.rearrange("p (cc i t) -> p cc t i", i=4, t=4),
+                a_nat[:, c, :, j0:j0 + 512].rearrange("p t (cc i) -> p cc t i", i=4),
+            )
+
+        def op_qadj(side, c, half):
+            j0 = half * 512
+            nc.vector.quantize_mx(
+                out=adj_codes[side][:, c, j0:j0 + 512].bitcast(FP8X4),
+                scales=adj_scales[side][:, c, j0:j0 + 512],
+                in_=adj_grp[side][:, (c * NODES + j0) * 4:(c * NODES + j0 + 512) * 4],
+            )
+
+        recip = [keep.tile([P, 8], F32, name="recip%d" % s) for s in range(2)]
+        recip01 = [keep.tile([P, 8], F32, name="recip01_%d" % s) for s in range(2)]
+        recip99 = [keep.tile([P, 8], F32, name="recip99_%d" % s) for s in range(2)]
+        d_in = keep.tile([P, 8], F32)
+
+        def finish_recip(side):
+            nc.vector.tensor_scalar_mul(out=recip01[side][:], in0=recip[side][:], scalar1=SLOPE)
+            nc.vector.tensor_scalar_mul(out=recip99[side][:], in0=recip[side][:], scalar1=1.0 - SLOPE)
+
+        def op_dout():
+            dps = psum.tile([P, 8, 32], F32, tag="bank")
+            for m in range(8):
+                for idx in range(8):
+                    nc.tensor.matmul(
+                        out=dps[:, m, :],
+                        lhsT=a_nat[:, idx // 4, idx % 4, m * P:(m + 1) * P],
+                        rhs=ones[:],
+                        start=(idx == 0),
+                        stop=(idx == 7),
+                    )
+            nc.vector.reciprocal(out=recip[0][:], in_=dps[:, :, 0])
+            finish_recip(0)
+
+        def op_din(c):
+            fps = psum.tile([P, 4, P], F32, tag="bank")
+            for t in range(4):
+                for s in range(8):
+                    nc.tensor.matmul(
+                        out=fps[:, t, :],
+                        lhsT=ident_b[:],
+                        rhs=a_nat[:, c, t, s * P:(s + 1) * P],
+                        start=(s == 0),
+                        stop=(s == 7),
+                    )
+            nc.vector.tensor_reduce(out=d_in[:, c * 4:(c + 1) * 4], in_=fps[:], axis=AX.X, op=ALU.add)
+
+        def op_dinf():
+            nc.vector.reciprocal(out=recip[1][:], in_=d_in[:])
+            finish_recip(1)
+
+        w_grp = {}
+        w_codes = {}
+        w_scales = {}
+
+        def op_s1(n):
+            unit, b = n // 8, n % 8
+            k, side = UNITS[unit]
+            c, dc = b // 4, b % 4
+            if b == 0:
+                w_grp[unit] = wpool.tile([P, 2, D, 4], BF16, tag="w_grp", align_bytes=64, name="w_grp%d" % unit)
+                w_codes[unit] = wpool.tile([P, 2, D], U32, tag="w_codes", bufs=4, align_bytes=64, name="w_codes%d" % unit)
+                w_scales[unit] = wpool.tile([P, 2, D], U8, tag="w_scales", bufs=4, align_bytes=64, name="w_scales%d" % unit)
+            s1 = psum.tile([P, 4, P], F32, tag="bank")
+            for t in range(4):
+                col = (c * 4 + t) * P
+                nc.tensor.matmul_mx(
+                    out=s1[:, t, :],
+                    lhsT=nt_codes[side][:, col:col + P].bitcast(FP8X4),
+                    lhsT_scale=nt_scales[side][:, col:col + P],
+                    rhs=wst_codes[:, k, dc * P:(dc + 1) * P].bitcast(FP8X4),
+                    rhs_scale=wst_scales[:, k, dc * P:(dc + 1) * P],
+                    start=True,
+                    stop=True,
+                )
+            nc.vector.tensor_tensor(
+                out=w_grp[unit][:, c, dc * P:(dc + 1) * P, :],
+                in0=s1[:].rearrange("p t d -> p d t"),
+                in1=bias_sb[:, k * D + dc * P:k * D + (dc + 1) * P].unsqueeze(2).to_broadcast([P, P, 4]),
+                op=ALU.add,
+            )
+
+        def op_qw(unit, c):
+            nc.vector.quantize_mx(
+                out=w_codes[unit][:, c, :].bitcast(FP8X4),
+                scales=w_scales[unit][:, c, :],
+                in_=w_grp[unit][:, c].rearrange("p d t -> p (d t)"),
+            )
+
+        q_rows = out_1.rearrange("k (c p t) d -> k c t p d", c=2, t=4)
+
+        def op_s2(n, path):
+            unit, m = n // 8, n % 8
+            k, side = UNITS[unit]
+            s2 = psum.tile([P, D], F32, tag="bank")
+            for c in range(2):
+                nc.tensor.matmul_mx(
+                    out=s2[:],
+                    lhsT=adj_codes[side][:, c, m * P:(m + 1) * P].bitcast(FP8X4),
+                    lhsT_scale=adj_scales[side][:, c, m * P:(m + 1) * P],
+                    rhs=w_codes[unit][:, c, :].bitcast(FP8X4),
+                    rhs_scale=w_scales[unit][:, c, :],
+                    start=(c == 0),
+                    stop=(c == 1),
+                )
+            o = outp.tile([P, D], F32, tag="o")
+            small = work.tile([P, D], F32, tag="small")
+            nc.scalar.activation(out=small[:], in_=s2[:], func=ACT.Copy, scale=recip01[side][:, m:m + 1])
+            if path == 1:
+                big = work.tile([P, D], F32, tag="big")
+                nc.scalar.activation(out=big[:], in_=s2[:], func=ACT.Relu, scale=recip99[side][:, m:m + 1])
+                nc.gpsimd.tensor_tensor(out=o[:], in0=big[:], in1=small[:], op=ALU.add)
+            else:
+                nc.vector.scalar_tensor_tensor(
+                    out=o[:], in0=s2[:], scalar=recip[side][:, m:m + 1], in1=small[:], op0=ALU.mult, op1=ALU.max
+                )
+            if side == 0:
+                nc.sync.dma_start(out=out_0[k, m * P:(m + 1) * P, :], in_=o[:])
+            else:
+                nc.sync.dma_start(out=q_rows[k, m // 4, m % 4], in_=o[:])
+
+        ops = {
+            "TB": op_tb, "QWS": op_qws, "QNT": op_qnt, "RG": op_rg, "QADJ": op_qadj, "DOUT": op_dout,
+            "DIN": op_din, "DINF": op_dinf, "S1": op_s1, "QW": op_qw, "S2": op_s2,
+        }
+        for step in PROGRAM:
+            ops[step[0]](*step[1:])

@@ -17,37 +17,36 @@ NODES = 1024
 D = 512
 K = 3
 SLOPE = 0.01
+GSPLIT = 1
 FLOPS = 2 * 2 * K * NODES * D * (D + NODES)
 
 UNITS = [(0, 0), (1, 0), (2, 0), (0, 1), (1, 1), (2, 1)]
 
 PROGRAM = [
-    ("TB", 0, 0, 0, 1), ("TB", 0, 0, 1, 0), ("TB", 1, 0, 0, 1), ("QWS", 0), ("TB", 1, 0, 1, 0), ("QNT", 0, 0),
-    ("TB", 1, 1, 0, 0), ("TB", 1, 1, 1, 1), ("QNT", 0, 1), ("S1", 0), ("S1", 1), ("RG", 0, 1, 0),
-    ("S1", 2), ("S1", 3), ("S1", 4), ("RG", 0, 0, 0), ("S1", 5), ("S1", 6),
-    ("S1", 7), ("QW", 0, 0), ("DIN", 0), ("QW", 0, 1), ("RG", 1, 0, 0), ("DOUT",),
-    ("RG", 1, 1, 0), ("QADJ", 0, 0, 1), ("QADJ", 0, 0, 0), ("QADJ", 0, 1, 0), ("QADJ", 0, 1, 1), ("TB", 0, 1, 1, 0),
-    ("TB", 0, 1, 0, 0), ("QWS", 1), ("TB", 0, 2, 1, 0), ("DIN", 1), ("TB", 0, 2, 0, 0), ("QWS", 2),
-    ("TB", 2, 1, 0, 0), ("S2", 0, 1), ("S1", 8), ("S1", 9), ("DINF",), ("S2", 1, 1),
-    ("S1", 10), ("S2", 2, 1), ("S1", 11), ("S1", 12), ("S1", 13), ("S1", 14),
-    ("S2", 3, 0), ("TB", 3, 1, 1, 0), ("S1", 15), ("QW", 1, 0), ("QW", 1, 1), ("S2", 4, 0),
-    ("S2", 5, 1), ("S2", 6, 1), ("S1", 16), ("S1", 17), ("S1", 18), ("S1", 19),
-    ("QW", 2, 0), ("TB", 2, 1, 1, 0), ("QNT", 1, 1), ("TB", 2, 0, 0, 0), ("TB", 2, 0, 1, 0), ("QNT", 1, 0),
-    ("S2", 7, 1), ("S2", 8, 0), ("S2", 9, 1), ("S1", 20), ("S1", 21), ("S1", 22),
-    ("S1", 23), ("QW", 2, 1), ("TB", 3, 0, 0, 0), ("TB", 3, 0, 2, 0), ("S2", 10, 1), ("S2", 11, 1),
-    ("S1", 24), ("S1", 25), ("S1", 26), ("S2", 12, 1), ("S1", 27), ("S1", 28),
-    ("S1", 29), ("S1", 30), ("S2", 13, 1), ("S1", 31), ("S2", 14, 0), ("S2", 15, 0),
-    ("S2", 16, 1), ("S1", 32), ("S1", 33), ("S1", 34), ("TB", 3, 0, 1, 0), ("QADJ", 1, 0, 0),
-    ("TB", 3, 1, 0, 0), ("QW", 3, 0), ("QADJ", 1, 1, 0), ("S2", 17, 0), ("S2", 18, 0), ("S2", 19, 1),
-    ("S2", 20, 1), ("S1", 35), ("S1", 36), ("S1", 37), ("TB", 3, 1, 2, 0), ("QW", 3, 1),
-    ("S1", 38), ("S2", 21, 0), ("TB", 3, 0, 3, 0), ("S2", 22, 1), ("S2", 23, 0), ("QADJ", 1, 0, 1),
-    ("TB", 3, 1, 3, 0), ("QADJ", 1, 1, 1), ("QW", 4, 0), ("S2", 24, 1), ("S2", 25, 0), ("S2", 26, 0),
-    ("S1", 39), ("S2", 27, 1), ("S1", 40), ("S1", 41), ("QW", 4, 1), ("S2", 28, 0),
-    ("S2", 29, 1), ("S1", 42), ("S1", 43), ("S2", 30, 0), ("S2", 31, 1), ("S2", 32, 0),
-    ("S2", 33, 1), ("S1", 44), ("S1", 45), ("S1", 46), ("S1", 47), ("S2", 34, 1),
-    ("S2", 35, 0), ("S2", 36, 0), ("QW", 5, 0), ("QW", 5, 1), ("S2", 37, 0), ("S2", 38, 0),
-    ("S2", 39, 1), ("S2", 40, 0), ("S2", 41, 0), ("S2", 42, 0), ("S2", 43, 0), ("S2", 44, 0),
-    ("S2", 45, 0), ("S2", 46, 0), ("S2", 47, 0),
+    ("TB", 0, 0, 0, 0), ("TB", 0, 0, 1, 0), ("TB", 1, 0, 0, 1), ("TB", 1, 0, 1, 0), ("QWS", 0), ("QNT", 0, 0, 1),
+    ("TB", 1, 1, 0, 0), ("RG", 0, 0, 0), ("TB", 1, 1, 1, 1), ("QNT", 0, 1, 1), ("S1", 0), ("S1", 1),
+    ("S1", 2), ("S1", 3), ("RG", 0, 1, 1), ("TB", 3, 1, 1, 0), ("S1", 4), ("S1", 5),
+    ("S1", 6), ("S1", 7), ("DIN", 0), ("RG", 1, 0, 0), ("TB", 0, 1, 1, 0), ("TB", 0, 2, 0, 0),
+    ("QW", 0), ("TB", 0, 1, 0, 0), ("QWS", 1), ("RG", 1, 1, 0), ("QADJ", 0, 0), ("DOUT",),
+    ("TB", 0, 2, 1, 0), ("TB", 2, 0, 0, 0), ("TB", 2, 0, 1, 0), ("QADJ", 0, 1), ("S1", 8), ("QWS", 2),
+    ("S1", 9), ("TB", 2, 1, 0, 0), ("S2", 0, 1), ("S2", 1, 1), ("S2", 2, 1), ("S1", 10),
+    ("S1", 11), ("S1", 12), ("S1", 13), ("S1", 14), ("S1", 15), ("S2", 3, 1),
+    ("S1", 16), ("S1", 17), ("S2", 4, 0), ("TB", 3, 1, 3, 0), ("QW", 1), ("S1", 18),
+    ("S2", 5, 1), ("S1", 19), ("S2", 6, 1), ("S2", 7, 1), ("S1", 20), ("S1", 21),
+    ("S1", 22), ("S1", 23), ("S2", 8, 0), ("S2", 9, 0), ("TB", 3, 0, 1, 0), ("TB", 2, 1, 1, 0),
+    ("QNT", 1, 0, 2), ("S2", 10, 0), ("TB", 3, 0, 0, 0), ("TB", 3, 1, 0, 0), ("QADJ", 1, 0), ("QW", 2),
+    ("S2", 11, 0), ("S2", 12, 1), ("S2", 13, 1), ("S2", 14, 1), ("DIN", 1), ("S1", 24),
+    ("S1", 25), ("S2", 15, 1), ("S2", 16, 1), ("S1", 26), ("S1", 27), ("S2", 17, 1),
+    ("S2", 18, 1), ("S1", 28), ("S1", 29), ("S2", 19, 1), ("S1", 30), ("S1", 31),
+    ("S1", 32), ("S1", 33), ("S1", 34), ("DINF",), ("S1", 35), ("S1", 36),
+    ("QW", 3), ("S2", 20, 0), ("S2", 21, 1), ("TB", 3, 1, 2, 0), ("S2", 22, 1), ("S1", 37),
+    ("S2", 23, 1), ("S1", 38), ("S1", 39), ("S1", 40), ("TB", 3, 0, 2, 0), ("TB", 3, 0, 3, 0),
+    ("S1", 41), ("QADJ", 1, 1), ("S2", 24, 1), ("S2", 25, 1), ("S1", 42), ("S1", 43),
+    ("S2", 26, 0), ("S2", 27, 0), ("QW", 4), ("S1", 44), ("S2", 28, 1), ("S2", 29, 0),
+    ("S2", 30, 1), ("S1", 45), ("S1", 46), ("S1", 47), ("S2", 31, 1), ("S2", 32, 0),
+    ("S2", 33, 0), ("S2", 34, 0), ("QW", 5), ("S2", 35, 0), ("S2", 36, 0), ("S2", 37, 0),
+    ("S2", 38, 1), ("S2", 39, 0), ("S2", 40, 0), ("S2", 41, 0), ("S2", 42, 0), ("S2", 43, 0),
+    ("S2", 44, 0), ("S2", 45, 0), ("S2", 46, 0), ("S2", 47, 0),
 ]
 
 
@@ -122,7 +121,9 @@ def tile_gglr_pa_kernel(tc, p_outgoing, q_incoming, adjacency_matrix, Ws, bs, ou
         adj_scales = [keep.tile([P, 2, NODES], U8, align_bytes=64, name="adj_scales%d" % s) for s in range(2)]
 
         def copy_on(eng, out, in_):
-            if eng == 0:
+            if eng == 2:
+                nc.gpsimd.tensor_scalar(out=out, in0=in_, scalar1=1.0, scalar2=0.0, op0=ALU.mult, op1=ALU.add)
+            elif eng == 0:
                 nc.scalar.copy(out=out, in_=in_)
             else:
                 nc.vector.tensor_copy(out=out, in_=in_)
@@ -143,7 +144,7 @@ def tile_gglr_pa_kernel(tc, p_outgoing, q_incoming, adjacency_matrix, Ws, bs, ou
                 for i in range(2):
                     m = 2 * b + i
                     words.append(a_nat[:, m // 4, m % 4, :].bitcast(F32)[:, a * 256:(a + 1) * 256])
-                tblock(words, adj_grp[1], a * NODES + b * 256, eng)
+                tblock(words, adj_grp[1], ((b // 2) * 2 + a) * 512 + (b % 2) * 256, eng)
             else:
                 nat = p_nat if kind == 1 else q_nat
                 tblock([nat[:, a, 2 * b + i, :].bitcast(F32) for i in range(2)], nt_grp[kind - 1], a * 512 + b * 256, eng)
@@ -155,28 +156,27 @@ def tile_gglr_pa_kernel(tc, p_outgoing, q_incoming, adjacency_matrix, Ws, bs, ou
                 in_=wst_grp[:, k * D * 4:(k + 1) * D * 4],
             )
 
-        def op_qnt(side, c):
+        def op_qnt(side, c, n):
             nc.vector.quantize_mx(
-                out=nt_codes[side][:, c * 512:(c + 1) * 512].bitcast(FP8X4),
-                scales=nt_scales[side][:, c * 512:(c + 1) * 512],
-                in_=nt_grp[side][:, c * 2048:(c + 1) * 2048],
+                out=nt_codes[side][:, c * 512:(c + n) * 512].bitcast(FP8X4),
+                scales=nt_scales[side][:, c * 512:(c + n) * 512],
+                in_=nt_grp[side][:, c * 2048:(c + n) * 2048],
             )
 
         def op_rg(c, half, eng):
             j0 = half * 512
-            dst = adj_grp[0][:, (c * NODES + j0) * 4:(c * NODES + j0 + 512) * 4]
+            dst = adj_grp[0][:, (half * 2 + c) * 2048:(half * 2 + c + 1) * 2048]
             copy_on(
                 eng,
                 dst.rearrange("p (cc i t) -> p cc t i", i=4, t=4),
                 a_nat[:, c, :, j0:j0 + 512].rearrange("p t (cc i) -> p cc t i", i=4),
             )
 
-        def op_qadj(side, c, half):
-            j0 = half * 512
+        def op_qadj(side, half):
             nc.vector.quantize_mx(
-                out=adj_codes[side][:, c, j0:j0 + 512].bitcast(FP8X4),
-                scales=adj_scales[side][:, c, j0:j0 + 512],
-                in_=adj_grp[side][:, (c * NODES + j0) * 4:(c * NODES + j0 + 512) * 4],
+                out=adj_codes[side][:, half, :].bitcast(FP8X4),
+                scales=adj_scales[side][:, half, :],
+                in_=adj_grp[side][:, half * 4096:(half + 1) * 4096],
             )
 
         recip = [keep.tile([P, 8], F32, name="recip%d" % s) for s in range(2)]
@@ -229,8 +229,8 @@ def tile_gglr_pa_kernel(tc, p_outgoing, q_incoming, adjacency_matrix, Ws, bs, ou
             c, dc = b // 4, b % 4
             if b == 0:
                 w_grp[unit] = wpool.tile([P, 2, D, 4], BF16, tag="w_grp", align_bytes=64, name="w_grp%d" % unit)
-                w_codes[unit] = wpool.tile([P, 2, D], U32, tag="w_codes", bufs=4, align_bytes=64, name="w_codes%d" % unit)
-                w_scales[unit] = wpool.tile([P, 2, D], U8, tag="w_scales", bufs=4, align_bytes=64, name="w_scales%d" % unit)
+                w_codes[unit] = wpool.tile([P, 2 * D], U32, tag="w_codes", bufs=4, align_bytes=64, name="w_codes%d" % unit)
+                w_scales[unit] = wpool.tile([P, 2 * D], U8, tag="w_scales", bufs=4, align_bytes=64, name="w_scales%d" % unit)
             s1 = psum.tile([P, 4, P], F32, tag="bank")
             for t in range(4):
                 col = (c * 4 + t) * P
@@ -250,11 +250,11 @@ def tile_gglr_pa_kernel(tc, p_outgoing, q_incoming, adjacency_matrix, Ws, bs, ou
                 op=ALU.add,
             )
 
-        def op_qw(unit, c):
+        def op_qw(unit):
             nc.vector.quantize_mx(
-                out=w_codes[unit][:, c, :].bitcast(FP8X4),
-                scales=w_scales[unit][:, c, :],
-                in_=w_grp[unit][:, c].rearrange("p d t -> p (d t)"),
+                out=w_codes[unit][:].bitcast(FP8X4),
+                scales=w_scales[unit][:],
+                in_=w_grp[unit][:].rearrange("p c d t -> p (c d t)"),
             )
 
         q_rows = out_1.rearrange("k (c p t) d -> k c t p d", c=2, t=4)
@@ -266,10 +266,10 @@ def tile_gglr_pa_kernel(tc, p_outgoing, q_incoming, adjacency_matrix, Ws, bs, ou
             for c in range(2):
                 nc.tensor.matmul_mx(
                     out=s2[:],
-                    lhsT=adj_codes[side][:, c, m * P:(m + 1) * P].bitcast(FP8X4),
-                    lhsT_scale=adj_scales[side][:, c, m * P:(m + 1) * P],
-                    rhs=w_codes[unit][:, c, :].bitcast(FP8X4),
-                    rhs_scale=w_scales[unit][:, c, :],
+                    lhsT=adj_codes[side][:, m // 4, c * 512 + (m % 4) * P:c * 512 + (m % 4 + 1) * P].bitcast(FP8X4),
+                    lhsT_scale=adj_scales[side][:, m // 4, c * 512 + (m % 4) * P:c * 512 + (m % 4 + 1) * P],
+                    rhs=w_codes[unit][:, c * D:(c + 1) * D].bitcast(FP8X4),
+                    rhs_scale=w_scales[unit][:, c * D:(c + 1) * D],
                     start=(c == 0),
                     stop=(c == 1),
                 )
@@ -279,7 +279,9 @@ def tile_gglr_pa_kernel(tc, p_outgoing, q_incoming, adjacency_matrix, Ws, bs, ou
             if path == 1:
                 big = work.tile([P, D], F32, tag="big")
                 nc.scalar.activation(out=big[:], in_=s2[:], func=ACT.Relu, scale=recip99[side][:, m:m + 1])
-                nc.gpsimd.tensor_tensor(out=o[:], in0=big[:], in1=small[:], op=ALU.add)
+                for g in range(GSPLIT):
+                    cols = slice(g * D // GSPLIT, (g + 1) * D // GSPLIT)
+                    nc.gpsimd.tensor_tensor(out=o[:, cols], in0=big[:, cols], in1=small[:, cols], op=ALU.add)
             else:
                 nc.vector.scalar_tensor_tensor(
                     out=o[:], in0=s2[:], scalar=recip[side][:, m:m + 1], in1=small[:], op0=ALU.mult, op1=ALU.max

@@ -13,41 +13,23 @@ ACT = mybir.ActivationFunctionType
 AX = mybir.AxisListType
 
 P = 128
+PACK = 4
+K_PASS = P * PACK
 NODES = 1024
 D = 512
-K = 3
+LAYERS = 3
+PASSES = NODES // K_PASS
+HALF = 512
 SLOPE = 0.01
-GSPLIT = 1
-FLOPS = 2 * 2 * K * NODES * D * (D + NODES)
+FLOPS = 2 * 2 * LAYERS * NODES * D * (D + NODES)
 
 UNITS = [(0, 0), (1, 0), (2, 0), (0, 1), (1, 1), (2, 1)]
-
-PROGRAM = [
-    ("TB", 0, 0, 0, 0), ("TB", 0, 0, 1, 0), ("TB", 1, 0, 0, 1), ("TB", 1, 0, 1, 0), ("QWS", 0), ("QNT", 0, 0, 1),
-    ("TB", 1, 1, 0, 0), ("RG", 0, 0, 0), ("TB", 1, 1, 1, 1), ("QNT", 0, 1, 1), ("S1", 0), ("S1", 1),
-    ("S1", 2), ("S1", 3), ("RG", 0, 1, 1), ("TB", 3, 1, 1, 0), ("S1", 4), ("S1", 5),
-    ("S1", 6), ("S1", 7), ("DIN", 0), ("RG", 1, 0, 0), ("TB", 0, 1, 1, 0), ("TB", 0, 2, 0, 0),
-    ("QW", 0), ("TB", 0, 1, 0, 0), ("QWS", 1), ("RG", 1, 1, 0), ("QADJ", 0, 0), ("DOUT",),
-    ("TB", 0, 2, 1, 0), ("TB", 2, 0, 0, 0), ("TB", 2, 0, 1, 0), ("QADJ", 0, 1), ("S1", 8), ("QWS", 2),
-    ("S1", 9), ("TB", 2, 1, 0, 0), ("S2", 0, 1), ("S2", 1, 1), ("S2", 2, 1), ("S1", 10),
-    ("S1", 11), ("S1", 12), ("S1", 13), ("S1", 14), ("S1", 15), ("S2", 3, 1),
-    ("S1", 16), ("S1", 17), ("S2", 4, 0), ("TB", 3, 1, 3, 0), ("QW", 1), ("S1", 18),
-    ("S2", 5, 1), ("S1", 19), ("S2", 6, 1), ("S2", 7, 1), ("S1", 20), ("S1", 21),
-    ("S1", 22), ("S1", 23), ("S2", 8, 0), ("S2", 9, 0), ("TB", 3, 0, 1, 0), ("TB", 2, 1, 1, 0),
-    ("QNT", 1, 0, 2), ("S2", 10, 0), ("TB", 3, 0, 0, 0), ("TB", 3, 1, 0, 0), ("QADJ", 1, 0), ("QW", 2),
-    ("S2", 11, 0), ("S2", 12, 1), ("S2", 13, 1), ("S2", 14, 1), ("DIN", 1), ("S1", 24),
-    ("S1", 25), ("S2", 15, 1), ("S2", 16, 1), ("S1", 26), ("S1", 27), ("S2", 17, 1),
-    ("S2", 18, 1), ("S1", 28), ("S1", 29), ("S2", 19, 1), ("S1", 30), ("S1", 31),
-    ("S1", 32), ("S1", 33), ("S1", 34), ("DINF",), ("S1", 35), ("S1", 36),
-    ("QW", 3), ("S2", 20, 0), ("S2", 21, 1), ("TB", 3, 1, 2, 0), ("S2", 22, 1), ("S1", 37),
-    ("S2", 23, 1), ("S1", 38), ("S1", 39), ("S1", 40), ("TB", 3, 0, 2, 0), ("TB", 3, 0, 3, 0),
-    ("S1", 41), ("QADJ", 1, 1), ("S2", 24, 1), ("S2", 25, 1), ("S1", 42), ("S1", 43),
-    ("S2", 26, 0), ("S2", 27, 0), ("QW", 4), ("S1", 44), ("S2", 28, 1), ("S2", 29, 0),
-    ("S2", 30, 1), ("S1", 45), ("S1", 46), ("S1", 47), ("S2", 31, 1), ("S2", 32, 0),
-    ("S2", 33, 0), ("S2", 34, 0), ("QW", 5), ("S2", 35, 0), ("S2", 36, 0), ("S2", 37, 0),
-    ("S2", 38, 1), ("S2", 39, 0), ("S2", 40, 0), ("S2", 41, 0), ("S2", 42, 0), ("S2", 43, 0),
-    ("S2", 44, 0), ("S2", 45, 0), ("S2", 46, 0), ("S2", 47, 0),
-]
+BANKS = 8
+N_BANKS = BANKS * len(UNITS)
+LEAD = 14
+GPSIMD_BANKS_END = 36
+LATER_START = 3
+LATER_STEP = 2
 
 
 def tile_gglr_pa_kernel(tc, p_outgoing, q_incoming, adjacency_matrix, Ws, bs, out_0, out_1):
@@ -60,42 +42,39 @@ def tile_gglr_pa_kernel(tc, p_outgoing, q_incoming, adjacency_matrix, Ws, bs, ou
         psum = ctx.enter_context(tc.psum_pool(name="psum", bufs=8))
         ctx.enter_context(tc.manual_schedule())
 
-        ident_f = keep.tile([P, P], F32)
-        make_identity(nc, ident_f[:])
-        ident_b = keep.tile([P, P], BF16)
-        make_identity(nc, ident_b[:])
+        ident_f32 = keep.tile([P, P], F32)
+        make_identity(nc, ident_f32[:])
+        ident_bf16 = keep.tile([P, P], BF16)
+        make_identity(nc, ident_bf16[:])
         ones = keep.tile([P, 32], BF16)
         nc.vector.memset(ones[:], 1.0)
-        bias_sb = keep.tile([P, K * D], BF16)
-        nc.scalar.dma_start(out=bias_sb[:], in_=bs.rearrange("k d -> (k d)").partition_broadcast(P))
+        bias = keep.tile([P, LAYERS * D], BF16)
+        nc.scalar.dma_start(out=bias[:], in_=bs.rearrange("k d -> (k d)").partition_broadcast(P))
 
-        ws_nat = keep.tile([P, K, 4, D], BF16)
-        p_nat = keep.tile([P, 2, 4, D], BF16)
-        q_nat = keep.tile([P, 2, 4, D], BF16)
-        a_nat = keep.tile([P, 2, 4, NODES], BF16)
+        ws_rows = keep.tile([P, LAYERS, PACK, D], BF16)
+        p_rows = keep.tile([P, PASSES, PACK, D], BF16)
+        q_rows = keep.tile([P, PASSES, PACK, D], BF16)
+        a_rows = keep.tile([P, PASSES, PACK, NODES], BF16)
 
         def load_ws(k, o0, o1):
             nc.sync.dma_start(
-                out=ws_nat[:, k, o0:o1],
-                in_=Ws[k, o0 * P:o1 * P, :].rearrange("(o r) i -> r o i", r=P),
+                out=ws_rows[:, k, o0:o1], in_=Ws[k, o0 * P:o1 * P, :].rearrange("(o r) i -> r o i", r=P)
             )
 
         def load_p(c, t0, t1):
-            nc.sync.dma_start(
-                out=p_nat[:, c, t0:t1],
-                in_=p_outgoing[c * 512:(c + 1) * 512, :].rearrange("(p t) d -> p t d", t=4)[:, t0:t1, :],
-            )
+            rows = p_outgoing[c * K_PASS:(c + 1) * K_PASS, :].rearrange("(p t) d -> p t d", t=PACK)
+            nc.sync.dma_start(out=p_rows[:, c, t0:t1], in_=rows[:, t0:t1, :])
 
         def load_q(g):
             nc.sync.dma_start(
-                out=q_nat[:, g].rearrange("p (u e) d -> p u e d", u=2),
-                in_=q_incoming[g * 512:(g + 1) * 512, :].rearrange("(u p e) d -> p u e d", u=2, e=2),
+                out=q_rows[:, g].rearrange("p (u e) d -> p u e d", u=2),
+                in_=q_incoming[g * K_PASS:(g + 1) * K_PASS, :].rearrange("(u p e) d -> p u e d", u=2, e=2),
             )
 
         def load_a(c):
             nc.sync.dma_start(
-                out=a_nat[:, c],
-                in_=adjacency_matrix[c * 512:(c + 1) * 512, :].rearrange("(p t) j -> p t j", t=4),
+                out=a_rows[:, c],
+                in_=adjacency_matrix[c * K_PASS:(c + 1) * K_PASS, :].rearrange("(p t) j -> p t j", t=PACK),
             )
 
         load_ws(0, 0, 2)
@@ -110,190 +89,252 @@ def tile_gglr_pa_kernel(tc, p_outgoing, q_incoming, adjacency_matrix, Ws, bs, ou
         load_q(0)
         load_q(1)
 
-        wst_grp = keep.tile([P, K * D * 4], BF16, align_bytes=64)
-        wst_codes = keep.tile([P, K, D], U32, align_bytes=64)
-        wst_scales = keep.tile([P, K, D], U8, align_bytes=64)
-        nt_grp = [keep.tile([P, NODES * 4], BF16, align_bytes=64, name="nt_grp%d" % s) for s in range(2)]
-        nt_codes = [keep.tile([P, NODES], U32, align_bytes=64, name="nt_codes%d" % s) for s in range(2)]
-        nt_scales = [keep.tile([P, NODES], U8, align_bytes=64, name="nt_scales%d" % s) for s in range(2)]
-        adj_grp = [keep.tile([P, 2 * NODES * 4], BF16, align_bytes=64, name="adj_grp%d" % s) for s in range(2)]
-        adj_codes = [keep.tile([P, 2, NODES], U32, align_bytes=64, name="adj_codes%d" % s) for s in range(2)]
-        adj_scales = [keep.tile([P, 2, NODES], U8, align_bytes=64, name="adj_scales%d" % s) for s in range(2)]
+        ws_grouped = keep.tile([P, LAYERS * D * PACK], BF16, align_bytes=64)
+        ws_codes = keep.tile([P, LAYERS, D], U32, align_bytes=64)
+        ws_scales = keep.tile([P, LAYERS, D], U8, align_bytes=64)
+        node_grouped = [keep.tile([P, NODES * PACK], BF16, align_bytes=64, name="node_grouped%d" % s) for s in range(2)]
+        node_codes = [keep.tile([P, NODES], U32, align_bytes=64, name="node_codes%d" % s) for s in range(2)]
+        node_scales = [keep.tile([P, NODES], U8, align_bytes=64, name="node_scales%d" % s) for s in range(2)]
+        adj_grouped = [keep.tile([P, PASSES * NODES * PACK], BF16, align_bytes=64, name="adj_grouped%d" % s) for s in range(2)]
+        adj_codes = [keep.tile([P, PASSES, NODES], U32, align_bytes=64, name="adj_codes%d" % s) for s in range(2)]
+        adj_scales = [keep.tile([P, PASSES, NODES], U8, align_bytes=64, name="adj_scales%d" % s) for s in range(2)]
 
-        def copy_on(eng, out, in_):
-            if eng == 2:
-                nc.gpsimd.tensor_scalar(out=out, in0=in_, scalar1=1.0, scalar2=0.0, op0=ALU.mult, op1=ALU.add)
-            elif eng == 0:
-                nc.scalar.copy(out=out, in_=in_)
-            else:
-                nc.vector.tensor_copy(out=out, in_=in_)
-
-        def tblock(words, grp, col0, eng):
-            tp = psum.tile([P, 2, 256], F32, tag="bank")
+        def transpose_two(tiles, grouped, col0, on_vector=False):
+            bank = psum.tile([P, 2, 2 * P], F32, tag="bank")
             for h in range(2):
+                words = tiles[h].bitcast(F32)
                 for u in range(2):
-                    nc.tensor.transpose(tp[:, u, h * P:(h + 1) * P], words[h][:, u * P:(u + 1) * P], ident_f[:])
-            dst = grp[:].bitcast(F32)[:, col0 * 2:(col0 + 256) * 2].rearrange("p (r u) -> p r u", u=2)
-            copy_on(eng, dst, tp[:].rearrange("p u r -> p r u"))
-
-        def op_tb(kind, a, b, eng):
-            if kind == 0:
-                tblock([ws_nat[:, a, 2 * b + i, :].bitcast(F32) for i in range(2)], wst_grp, a * D + b * 256, eng)
-            elif kind == 3:
-                words = []
-                for i in range(2):
-                    m = 2 * b + i
-                    words.append(a_nat[:, m // 4, m % 4, :].bitcast(F32)[:, a * 256:(a + 1) * 256])
-                tblock(words, adj_grp[1], ((b // 2) * 2 + a) * 512 + (b % 2) * 256, eng)
+                    nc.tensor.transpose(bank[:, u, h * P:(h + 1) * P], words[:, u * P:(u + 1) * P], ident_f32[:])
+            dst = grouped[:].bitcast(F32)[:, col0 * 2:(col0 + 2 * P) * 2].rearrange("p (r u) -> p r u", u=2)
+            src = bank[:].rearrange("p u r -> p r u")
+            if on_vector:
+                nc.vector.tensor_copy(out=dst, in_=src)
             else:
-                nat = p_nat if kind == 1 else q_nat
-                tblock([nat[:, a, 2 * b + i, :].bitcast(F32) for i in range(2)], nt_grp[kind - 1], a * 512 + b * 256, eng)
+                nc.scalar.copy(out=dst, in_=src)
 
-        def op_qws(k):
+        def transpose_weights(k, share_with_vector=False):
+            for h in range(2):
+                tiles = [ws_rows[:, k, 2 * h + i, :] for i in range(2)]
+                transpose_two(tiles, ws_grouped, k * D + h * 2 * P, on_vector=share_with_vector and h == 1)
+
+        def quantise_weights(k):
             nc.vector.quantize_mx(
-                out=wst_codes[:, k, :].bitcast(FP8X4),
-                scales=wst_scales[:, k, :],
-                in_=wst_grp[:, k * D * 4:(k + 1) * D * 4],
+                out=ws_codes[:, k, :].bitcast(FP8X4),
+                scales=ws_scales[:, k, :],
+                in_=ws_grouped[:, k * D * PACK:(k + 1) * D * PACK],
             )
 
-        def op_qnt(side, c, n):
+        def transpose_nodes(side, c, share_with_vector=False):
+            rows = p_rows if side == 0 else q_rows
+            for h in range(2):
+                tiles = [rows[:, c, 2 * h + i, :] for i in range(2)]
+                transpose_two(tiles, node_grouped[side], c * K_PASS + h * 2 * P, on_vector=share_with_vector and h == 1)
+
+        def quantise_nodes(side, c):
+            cols = slice(c * K_PASS, (c + 1) * K_PASS)
             nc.vector.quantize_mx(
-                out=nt_codes[side][:, c * 512:(c + n) * 512].bitcast(FP8X4),
-                scales=nt_scales[side][:, c * 512:(c + n) * 512],
-                in_=nt_grp[side][:, c * 2048:(c + n) * 2048],
+                out=node_codes[side][:, cols].bitcast(FP8X4),
+                scales=node_scales[side][:, cols],
+                in_=node_grouped[side][:, c * K_PASS * PACK:(c + 1) * K_PASS * PACK],
             )
 
-        def op_rg(c, half, eng):
-            j0 = half * 512
-            dst = adj_grp[0][:, (half * 2 + c) * 2048:(half * 2 + c + 1) * 2048]
-            copy_on(
-                eng,
-                dst.rearrange("p (cc i t) -> p cc t i", i=4, t=4),
-                a_nat[:, c, :, j0:j0 + 512].rearrange("p t (cc i) -> p cc t i", i=4),
+        def regroup_adjacency(c, half):
+            j0 = half * HALF
+            dst = adj_grouped[0][:, (c * NODES + j0) * PACK:(c * NODES + j0 + HALF) * PACK]
+            nc.scalar.copy(
+                out=dst.rearrange("p (b i t) -> p b t i", i=4, t=PACK),
+                in_=a_rows[:, c, :, j0:j0 + HALF].rearrange("p t (b i) -> p b t i", i=4),
             )
 
-        def op_qadj(side, half):
+        def transpose_adjacency(g, half):
+            for pair in range(2 * half, 2 * half + 2):
+                tiles = []
+                for m in range(2 * pair, 2 * pair + 2):
+                    tiles.append(a_rows[:, m // PACK, m % PACK, g * K_PASS:(g + 1) * K_PASS])
+                transpose_two(tiles, adj_grouped[1], g * NODES + pair * 2 * P)
+
+        def quantise_adjacency(side, c, half):
+            j0 = half * HALF
             nc.vector.quantize_mx(
-                out=adj_codes[side][:, half, :].bitcast(FP8X4),
-                scales=adj_scales[side][:, half, :],
-                in_=adj_grp[side][:, half * 4096:(half + 1) * 4096],
+                out=adj_codes[side][:, c, j0:j0 + HALF].bitcast(FP8X4),
+                scales=adj_scales[side][:, c, j0:j0 + HALF],
+                in_=adj_grouped[side][:, (c * NODES + j0) * PACK:(c * NODES + j0 + HALF) * PACK],
             )
 
-        recip = [keep.tile([P, 8], F32, name="recip%d" % s) for s in range(2)]
-        recip01 = [keep.tile([P, 8], F32, name="recip01_%d" % s) for s in range(2)]
-        recip99 = [keep.tile([P, 8], F32, name="recip99_%d" % s) for s in range(2)]
-        d_in = keep.tile([P, 8], F32)
+        recip = [keep.tile([P, BANKS], F32, name="recip%d" % s) for s in range(2)]
+        recip_small = [keep.tile([P, BANKS], F32, name="recip_small%d" % s) for s in range(2)]
+        recip_big = [keep.tile([P, BANKS], F32, name="recip_big%d" % s) for s in range(2)]
+        d_in = keep.tile([P, BANKS], F32)
 
-        def finish_recip(side):
-            nc.vector.tensor_scalar_mul(out=recip01[side][:], in0=recip[side][:], scalar1=SLOPE)
-            nc.vector.tensor_scalar_mul(out=recip99[side][:], in0=recip[side][:], scalar1=1.0 - SLOPE)
+        def scaled_reciprocals(side):
+            nc.vector.tensor_scalar_mul(out=recip_small[side][:], in0=recip[side][:], scalar1=SLOPE)
+            nc.vector.tensor_scalar_mul(out=recip_big[side][:], in0=recip[side][:], scalar1=1.0 - SLOPE)
 
-        def op_dout():
-            dps = psum.tile([P, 8, 32], F32, tag="bank")
-            for m in range(8):
-                for idx in range(8):
+        def degree_out():
+            sums = psum.tile([P, BANKS, 32], F32, tag="bank")
+            for m in range(BANKS):
+                for r in range(BANKS):
                     nc.tensor.matmul(
-                        out=dps[:, m, :],
-                        lhsT=a_nat[:, idx // 4, idx % 4, m * P:(m + 1) * P],
+                        out=sums[:, m, :],
+                        lhsT=a_rows[:, r // PACK, r % PACK, m * P:(m + 1) * P],
                         rhs=ones[:],
-                        start=(idx == 0),
-                        stop=(idx == 7),
+                        start=(r == 0),
+                        stop=(r == BANKS - 1),
                     )
-            nc.vector.reciprocal(out=recip[0][:], in_=dps[:, :, 0])
-            finish_recip(0)
+            nc.vector.reciprocal(out=recip[0][:], in_=sums[:, :, 0])
+            scaled_reciprocals(0)
 
-        def op_din(c):
-            fps = psum.tile([P, 4, P], F32, tag="bank")
-            for t in range(4):
-                for s in range(8):
+        def degree_in(c):
+            folded = psum.tile([P, PACK, P], F32, tag="bank")
+            for t in range(PACK):
+                for s in range(NODES // P):
                     nc.tensor.matmul(
-                        out=fps[:, t, :],
-                        lhsT=ident_b[:],
-                        rhs=a_nat[:, c, t, s * P:(s + 1) * P],
+                        out=folded[:, t, :],
+                        lhsT=ident_bf16[:],
+                        rhs=a_rows[:, c, t, s * P:(s + 1) * P],
                         start=(s == 0),
-                        stop=(s == 7),
+                        stop=(s == NODES // P - 1),
                     )
-            nc.vector.tensor_reduce(out=d_in[:, c * 4:(c + 1) * 4], in_=fps[:], axis=AX.X, op=ALU.add)
+            nc.vector.tensor_reduce(out=d_in[:, c * PACK:(c + 1) * PACK], in_=folded[:], axis=AX.X, op=ALU.add)
 
-        def op_dinf():
+        def degree_in_reciprocals():
             nc.vector.reciprocal(out=recip[1][:], in_=d_in[:])
-            finish_recip(1)
+            scaled_reciprocals(1)
 
-        w_grp = {}
+        w_grouped = {}
         w_codes = {}
         w_scales = {}
 
-        def op_s1(n):
-            unit, b = n // 8, n % 8
+        def stage1_bank(n):
+            unit, b = n // BANKS, n % BANKS
             k, side = UNITS[unit]
-            c, dc = b // 4, b % 4
+            c, f = b // PACK, b % PACK
             if b == 0:
-                w_grp[unit] = wpool.tile([P, 2, D, 4], BF16, tag="w_grp", align_bytes=64, name="w_grp%d" % unit)
-                w_codes[unit] = wpool.tile([P, 2 * D], U32, tag="w_codes", bufs=4, align_bytes=64, name="w_codes%d" % unit)
-                w_scales[unit] = wpool.tile([P, 2 * D], U8, tag="w_scales", bufs=4, align_bytes=64, name="w_scales%d" % unit)
-            s1 = psum.tile([P, 4, P], F32, tag="bank")
-            for t in range(4):
-                col = (c * 4 + t) * P
+                w_grouped[unit] = wpool.tile([P, PASSES, D, PACK], BF16, tag="w_grouped", align_bytes=64, name="w_grouped%d" % unit)
+                w_codes[unit] = wpool.tile([P, PASSES, D], U32, tag="w_codes", bufs=4, align_bytes=64, name="w_codes%d" % unit)
+                w_scales[unit] = wpool.tile([P, PASSES, D], U8, tag="w_scales", bufs=4, align_bytes=64, name="w_scales%d" % unit)
+            feats = slice(f * P, (f + 1) * P)
+            bank = psum.tile([P, PACK, P], F32, tag="bank")
+            for t in range(PACK):
+                nodes = slice((c * PACK + t) * P, (c * PACK + t + 1) * P)
                 nc.tensor.matmul_mx(
-                    out=s1[:, t, :],
-                    lhsT=nt_codes[side][:, col:col + P].bitcast(FP8X4),
-                    lhsT_scale=nt_scales[side][:, col:col + P],
-                    rhs=wst_codes[:, k, dc * P:(dc + 1) * P].bitcast(FP8X4),
-                    rhs_scale=wst_scales[:, k, dc * P:(dc + 1) * P],
+                    out=bank[:, t, :],
+                    lhsT=node_codes[side][:, nodes].bitcast(FP8X4),
+                    lhsT_scale=node_scales[side][:, nodes],
+                    rhs=ws_codes[:, k, feats].bitcast(FP8X4),
+                    rhs_scale=ws_scales[:, k, feats],
                     start=True,
                     stop=True,
                 )
             nc.vector.tensor_tensor(
-                out=w_grp[unit][:, c, dc * P:(dc + 1) * P, :],
-                in0=s1[:].rearrange("p t d -> p d t"),
-                in1=bias_sb[:, k * D + dc * P:k * D + (dc + 1) * P].unsqueeze(2).to_broadcast([P, P, 4]),
+                out=w_grouped[unit][:, c, feats, :],
+                in0=bank[:].rearrange("p t d -> p d t"),
+                in1=bias[:, k * D + f * P:k * D + (f + 1) * P].unsqueeze(2).to_broadcast([P, P, PACK]),
                 op=ALU.add,
             )
 
-        def op_qw(unit):
+        def quantise_stage1(unit, c):
             nc.vector.quantize_mx(
-                out=w_codes[unit][:].bitcast(FP8X4),
-                scales=w_scales[unit][:],
-                in_=w_grp[unit][:].rearrange("p c d t -> p (c d t)"),
+                out=w_codes[unit][:, c, :].bitcast(FP8X4),
+                scales=w_scales[unit][:, c, :],
+                in_=w_grouped[unit][:, c].rearrange("p d t -> p (d t)"),
             )
 
-        q_rows = out_1.rearrange("k (c p t) d -> k c t p d", c=2, t=4)
+        q_out = out_1.rearrange("k (c p t) d -> k c t p d", c=PASSES, t=PACK)
 
-        def op_s2(n, path):
-            unit, m = n // 8, n % 8
+        def stage2_bank(n):
+            unit, m = n // BANKS, n % BANKS
             k, side = UNITS[unit]
-            s2 = psum.tile([P, D], F32, tag="bank")
-            for c in range(2):
+            nodes = slice(m * P, (m + 1) * P)
+            bank = psum.tile([P, D], F32, tag="bank")
+            for c in range(PASSES):
                 nc.tensor.matmul_mx(
-                    out=s2[:],
-                    lhsT=adj_codes[side][:, m // 4, c * 512 + (m % 4) * P:c * 512 + (m % 4 + 1) * P].bitcast(FP8X4),
-                    lhsT_scale=adj_scales[side][:, m // 4, c * 512 + (m % 4) * P:c * 512 + (m % 4 + 1) * P],
-                    rhs=w_codes[unit][:, c * D:(c + 1) * D].bitcast(FP8X4),
-                    rhs_scale=w_scales[unit][:, c * D:(c + 1) * D],
+                    out=bank[:],
+                    lhsT=adj_codes[side][:, c, nodes].bitcast(FP8X4),
+                    lhsT_scale=adj_scales[side][:, c, nodes],
+                    rhs=w_codes[unit][:, c, :].bitcast(FP8X4),
+                    rhs_scale=w_scales[unit][:, c, :],
                     start=(c == 0),
-                    stop=(c == 1),
+                    stop=(c == PASSES - 1),
                 )
-            o = outp.tile([P, D], F32, tag="o")
+            result = outp.tile([P, D], F32, tag="result")
             small = work.tile([P, D], F32, tag="small")
-            nc.scalar.activation(out=small[:], in_=s2[:], func=ACT.Copy, scale=recip01[side][:, m:m + 1])
-            if path == 1:
+            nc.scalar.activation(out=small[:], in_=bank[:], func=ACT.Copy, scale=recip_small[side][:, m:m + 1])
+            if n % 2 == 1 and n < GPSIMD_BANKS_END:
                 big = work.tile([P, D], F32, tag="big")
-                nc.scalar.activation(out=big[:], in_=s2[:], func=ACT.Relu, scale=recip99[side][:, m:m + 1])
-                for g in range(GSPLIT):
-                    cols = slice(g * D // GSPLIT, (g + 1) * D // GSPLIT)
-                    nc.gpsimd.tensor_tensor(out=o[:, cols], in0=big[:, cols], in1=small[:, cols], op=ALU.add)
+                nc.scalar.activation(out=big[:], in_=bank[:], func=ACT.Relu, scale=recip_big[side][:, m:m + 1])
+                nc.gpsimd.tensor_tensor(out=result[:], in0=big[:], in1=small[:], op=ALU.add)
             else:
                 nc.vector.scalar_tensor_tensor(
-                    out=o[:], in0=s2[:], scalar=recip[side][:, m:m + 1], in1=small[:], op0=ALU.mult, op1=ALU.max
+                    out=result[:], in0=bank[:], scalar=recip[side][:, m:m + 1], in1=small[:], op0=ALU.mult, op1=ALU.max
                 )
             if side == 0:
-                nc.sync.dma_start(out=out_0[k, m * P:(m + 1) * P, :], in_=o[:])
+                nc.sync.dma_start(out=out_0[k, nodes, :], in_=result[:])
             else:
-                nc.sync.dma_start(out=q_rows[k, m // 4, m % 4], in_=o[:])
+                nc.sync.dma_start(out=q_out[k, m // PACK, m % PACK], in_=result[:])
 
-        ops = {
-            "TB": op_tb, "QWS": op_qws, "QNT": op_qnt, "RG": op_rg, "QADJ": op_qadj, "DOUT": op_dout,
-            "DIN": op_din, "DINF": op_dinf, "S1": op_s1, "QW": op_qw, "S2": op_s2,
-        }
-        for step in PROGRAM:
-            ops[step[0]](*step[1:])
+        transpose_weights(0, share_with_vector=True)
+        transpose_nodes(0, 0, share_with_vector=True)
+        quantise_weights(0)
+        quantise_nodes(0, 0)
+        transpose_nodes(0, 1, share_with_vector=True)
+        quantise_nodes(0, 1)
+        for n in range(0, 2):
+            stage1_bank(n)
+        regroup_adjacency(0, 0)
+        for n in range(2, 5):
+            stage1_bank(n)
+        regroup_adjacency(0, 1)
+        for n in range(5, BANKS):
+            stage1_bank(n)
+        quantise_stage1(0, 0)
+        degree_in(0)
+        quantise_stage1(0, 1)
+        regroup_adjacency(1, 0)
+        degree_out()
+        regroup_adjacency(1, 1)
+        for c in range(PASSES):
+            for half in range(2):
+                quantise_adjacency(0, c, half)
+        transpose_weights(1)
+        quantise_weights(1)
+        transpose_weights(2)
+        degree_in(1)
+        quantise_weights(2)
+        degree_in_reciprocals()
+
+        later = [
+            lambda: transpose_nodes(1, 0),
+            lambda: transpose_nodes(1, 1),
+            lambda: quantise_nodes(1, 0),
+            lambda: quantise_nodes(1, 1),
+            lambda: transpose_adjacency(0, 0),
+            lambda: transpose_adjacency(1, 0),
+            lambda: quantise_adjacency(1, 0, 0),
+            lambda: quantise_adjacency(1, 1, 0),
+            lambda: transpose_adjacency(0, 1),
+            lambda: transpose_adjacency(1, 1),
+            lambda: quantise_adjacency(1, 0, 1),
+            lambda: quantise_adjacency(1, 1, 1),
+        ]
+
+        done1 = BANKS
+        done_later = 0
+        to_quantise = []
+        for n in range(N_BANKS):
+            stage2_bank(n)
+            while done1 < min(N_BANKS, n + LEAD):
+                stage1_bank(done1)
+                done1 += 1
+                for unit, c in to_quantise:
+                    quantise_stage1(unit, c)
+                to_quantise = []
+                if done1 % PACK == 0:
+                    to_quantise.append(((done1 - 1) // BANKS, ((done1 - 1) % BANKS) // PACK))
+            if done1 == N_BANKS:
+                for unit, c in to_quantise:
+                    quantise_stage1(unit, c)
+                to_quantise = []
+            if n >= LATER_START and (n - LATER_START) % LATER_STEP == 0 and done_later < len(later):
+                later[done_later]()
+                done_later += 1

@@ -26,10 +26,10 @@ FLOPS = 2 * 2 * LAYERS * NODES * D * (D + NODES)
 UNITS = [(0, 0), (1, 0), (2, 0), (0, 1), (1, 1), (2, 1)]
 BANKS = 8
 N_BANKS = BANKS * len(UNITS)
-LEAD = 14
-GPSIMD_BANKS_END = 36
-LATER_START = 3
-LATER_STEP = 2
+BLOCK = 4
+ROUNDS = N_BANKS // BLOCK
+LEAD_BLOCKS = 3
+GPSIMD_ROUNDS = 9
 
 
 def tile_gglr_pa_kernel(tc, p_outgoing, q_incoming, adjacency_matrix, Ws, bs, out_0, out_1):
@@ -260,7 +260,7 @@ def tile_gglr_pa_kernel(tc, p_outgoing, q_incoming, adjacency_matrix, Ws, bs, ou
             result = outp.tile([P, D], F32, tag="result")
             small = work.tile([P, D], F32, tag="small")
             nc.scalar.activation(out=small[:], in_=bank[:], func=ACT.Copy, scale=recip_small[side][:, m:m + 1])
-            if n % 2 == 1 and n < GPSIMD_BANKS_END:
+            if n % 2 == 1 and n // BLOCK < GPSIMD_ROUNDS:
                 big = work.tile([P, D], F32, tag="big")
                 nc.scalar.activation(out=big[:], in_=bank[:], func=ACT.Relu, scale=recip_big[side][:, m:m + 1])
                 nc.gpsimd.tensor_tensor(out=result[:], in0=big[:], in1=small[:], op=ALU.add)
@@ -303,38 +303,42 @@ def tile_gglr_pa_kernel(tc, p_outgoing, q_incoming, adjacency_matrix, Ws, bs, ou
         quantise_weights(2)
         degree_in_reciprocals()
 
-        later = [
+        def stage1_block(b):
+            for n in range(b * BLOCK, (b + 1) * BLOCK):
+                stage1_bank(n)
+
+        def quantise_block(b):
+            quantise_stage1(b // PASSES, b % PASSES)
+
+        later_transposes = [
             lambda: transpose_nodes(1, 0),
             lambda: transpose_nodes(1, 1),
-            lambda: quantise_nodes(1, 0),
-            lambda: quantise_nodes(1, 1),
             lambda: transpose_adjacency(0, 0),
             lambda: transpose_adjacency(1, 0),
-            lambda: quantise_adjacency(1, 0, 0),
-            lambda: quantise_adjacency(1, 1, 0),
             lambda: transpose_adjacency(0, 1),
             lambda: transpose_adjacency(1, 1),
+        ]
+        later_quantises = [
+            lambda: quantise_nodes(1, 0),
+            lambda: quantise_nodes(1, 1),
+            lambda: quantise_adjacency(1, 0, 0),
+            lambda: quantise_adjacency(1, 1, 0),
             lambda: quantise_adjacency(1, 0, 1),
             lambda: quantise_adjacency(1, 1, 1),
         ]
 
-        done1 = BANKS
-        done_later = 0
-        to_quantise = []
-        for n in range(N_BANKS):
-            stage2_bank(n)
-            while done1 < min(N_BANKS, n + LEAD):
-                stage1_bank(done1)
-                done1 += 1
-                for unit, c in to_quantise:
-                    quantise_stage1(unit, c)
-                to_quantise = []
-                if done1 % PACK == 0:
-                    to_quantise.append(((done1 - 1) // BANKS, ((done1 - 1) % BANKS) // PACK))
-            if done1 == N_BANKS:
-                for unit, c in to_quantise:
-                    quantise_stage1(unit, c)
-                to_quantise = []
-            if n >= LATER_START and (n - LATER_START) % LATER_STEP == 0 and done_later < len(later):
-                later[done_later]()
-                done_later += 1
+        stage1_block(LEAD_BLOCKS - 1)
+        later_transposes[0]()
+        quantise_block(LEAD_BLOCKS - 1)
+        for r in range(ROUNDS):
+            for n in range(r * BLOCK, (r + 1) * BLOCK):
+                stage2_bank(n)
+            ahead = r + LEAD_BLOCKS
+            if ahead < ROUNDS:
+                stage1_block(ahead)
+            if r + 1 < len(later_transposes):
+                later_transposes[r + 1]()
+            if r < len(later_quantises):
+                later_quantises[r]()
+            if ahead < ROUNDS:
+                quantise_block(ahead)

@@ -260,7 +260,7 @@ def tile_gglr_pa_kernel(tc, p_outgoing, q_incoming, adjacency_matrix, Ws, bs, ou
             result = outp.tile([P, D], F32, tag="result")
             small = work.tile([P, D], F32, tag="small")
             nc.scalar.activation(out=small[:], in_=bank[:], func=ACT.Copy, scale=recip_small[side][:, m:m + 1])
-            if n % 2 == 1 and n // BLOCK < GPSIMD_ROUNDS:
+            if n % BLOCK < 2 and n // BLOCK < GPSIMD_ROUNDS:
                 big = work.tile([P, D], F32, tag="big")
                 nc.scalar.activation(out=big[:], in_=bank[:], func=ACT.Relu, scale=recip_big[side][:, m:m + 1])
                 nc.gpsimd.tensor_tensor(out=result[:], in0=big[:], in1=small[:], op=ALU.add)
@@ -331,11 +331,14 @@ def tile_gglr_pa_kernel(tc, p_outgoing, q_incoming, adjacency_matrix, Ws, bs, ou
         later_transposes[0]()
         quantise_block(LEAD_BLOCKS - 1)
         for r in range(ROUNDS):
-            for n in range(r * BLOCK, (r + 1) * BLOCK):
-                stage2_bank(n)
+            first = r * BLOCK
             ahead = r + LEAD_BLOCKS
+            stage2_bank(first)
+            stage2_bank(first + 1)
             if ahead < ROUNDS:
                 stage1_block(ahead)
+            stage2_bank(first + 2)
+            stage2_bank(first + 3)
             if r + 1 < len(later_transposes):
                 later_transposes[r + 1]()
             if r < len(later_quantises):

@@ -46,10 +46,12 @@ def tile_gglr_pa_kernel(tc, p_outgoing, q_incoming, adjacency_matrix, Ws, bs, ou
         make_identity(nc, ident_f32[:])
         ident_bf16 = keep.tile([P, P], BF16)
         make_identity(nc, ident_bf16[:])
-        ones = keep.tile([P, 32], BF16)
+        ones = keep.tile([P, P], BF16)
         nc.vector.memset(ones[:], 1.0)
+        bias_row = keep.tile([P, LAYERS * D], BF16)
+        nc.vector.memset(bias_row[:], 0.0)
+        nc.scalar.dma_start(out=bias_row[0:1, :], in_=bs.rearrange("(o k) d -> o (k d)", o=1))
         bias = keep.tile([P, LAYERS * D], BF16)
-        nc.scalar.dma_start(out=bias[:], in_=bs.rearrange("k d -> (k d)").partition_broadcast(P))
 
         ws_rows = keep.tile([P, LAYERS, PACK, D], BF16)
         p_rows = keep.tile([P, PASSES, PACK, D], BF16)
@@ -161,6 +163,13 @@ def tile_gglr_pa_kernel(tc, p_outgoing, q_incoming, adjacency_matrix, Ws, bs, ou
                 in_=adj_grouped[side][:, (c * NODES + j0) * PACK:(c * NODES + j0 + HALF) * PACK],
             )
 
+        def spread_bias():
+            for k in range(LAYERS):
+                feats = slice(k * D, (k + 1) * D)
+                bank = psum.tile([P, D], F32, tag="bank")
+                nc.tensor.matmul(out=bank[:], lhsT=ones[:], rhs=bias_row[:, feats], start=True, stop=True)
+                nc.scalar.copy(out=bias[:, feats], in_=bank[:])
+
         recip = [keep.tile([P, BANKS], F32, name="recip%d" % s) for s in range(2)]
         recip_small = [keep.tile([P, BANKS], F32, name="recip_small%d" % s) for s in range(2)]
         recip_big = [keep.tile([P, BANKS], F32, name="recip_big%d" % s) for s in range(2)]
@@ -177,7 +186,7 @@ def tile_gglr_pa_kernel(tc, p_outgoing, q_incoming, adjacency_matrix, Ws, bs, ou
                     nc.tensor.matmul(
                         out=sums[:, m, :],
                         lhsT=a_rows[:, r // PACK, r % PACK, m * P:(m + 1) * P],
-                        rhs=ones[:],
+                        rhs=ones[:, 0:32],
                         start=(r == 0),
                         stop=(r == BANKS - 1),
                     )
@@ -278,6 +287,7 @@ def tile_gglr_pa_kernel(tc, p_outgoing, q_incoming, adjacency_matrix, Ws, bs, ou
         quantise_weights(0)
         quantise_nodes(0, 0)
         transpose_nodes(0, 1, share_with_vector=True)
+        spread_bias()
         quantise_nodes(0, 1)
         for n in range(0, 2):
             stage1_bank(n)

@@ -8,6 +8,7 @@ BF16 = mybir.dt.bfloat16
 F32 = mybir.dt.float32
 U32 = mybir.dt.uint32
 U8 = mybir.dt.uint8
+I32 = mybir.dt.int32
 ALU = mybir.AluOpType
 ACT = mybir.ActivationFunctionType
 AX = mybir.AxisListType
@@ -46,11 +47,10 @@ def tile_gglr_pa_kernel(tc, p_outgoing, q_incoming, adjacency_matrix, Ws, bs, ou
         make_identity(nc, ident_f32[:])
         ident_bf16 = keep.tile([P, P], BF16)
         make_identity(nc, ident_bf16[:])
+        bias_row = keep.tile([P, LAYERS * D], BF16)
+        nc.vector.memset(bias_row[:].bitcast(I32), 0)
         ones = keep.tile([P, P], BF16)
         nc.vector.memset(ones[:], 1.0)
-        bias_row = keep.tile([P, LAYERS * D], BF16)
-        nc.vector.memset(bias_row[:], 0.0)
-        nc.scalar.dma_start(out=bias_row[0:1, :], in_=bs.rearrange("(o k) d -> o (k d)", o=1))
         bias = keep.tile([P, LAYERS * D], BF16)
 
         ws_rows = keep.tile([P, LAYERS, PACK, D], BF16)
@@ -80,6 +80,7 @@ def tile_gglr_pa_kernel(tc, p_outgoing, q_incoming, adjacency_matrix, Ws, bs, ou
             )
 
         load_ws(0, 0, 2)
+        nc.sync.dma_start(out=bias_row[0:1, :], in_=bs.rearrange("(o k) d -> o (k d)", o=1))
         load_ws(0, 2, 4)
         load_p(0, 0, 2)
         load_p(0, 2, 4)

@@ -181,13 +181,13 @@ def tile_gglr_pa_kernel(tc, p_outgoing, q_incoming, adjacency_matrix, Ws, bs, ou
             nc.vector.tensor_scalar_mul(out=recip_big[side][:], in0=recip[side][:], scalar1=1.0 - SLOPE)
 
         def degree_out():
-            sums = psum.tile([P, BANKS, 32], F32, tag="bank")
+            sums = psum.tile([P, BANKS, 64], F32, tag="bank")
             for m in range(BANKS):
                 for r in range(BANKS):
                     nc.tensor.matmul(
                         out=sums[:, m, :],
                         lhsT=a_rows[:, r // PACK, r % PACK, m * P:(m + 1) * P],
-                        rhs=ones[:, 0:32],
+                        rhs=ones[:, 0:64],
                         start=(r == 0),
                         stop=(r == BANKS - 1),
                     )

@@ -40,7 +40,7 @@ def tile_gglr_pa_kernel(tc, p_outgoing, q_incoming, adjacency_matrix, Ws, bs, ou
         wpool = ctx.enter_context(tc.tile_pool(name="wpool", bufs=2))
         work = ctx.enter_context(tc.tile_pool(name="work", bufs=4))
         outp = ctx.enter_context(tc.tile_pool(name="outp", bufs=6))
-        psum = ctx.enter_context(tc.psum_pool(name="psum", bufs=8))
+        psum = ctx.enter_context(tc.psum_pool(name="psum", bufs=7))
         ctx.enter_context(tc.manual_schedule())
 
         ident_f32 = keep.tile([P, P], F32)
@@ -141,13 +141,14 @@ def tile_gglr_pa_kernel(tc, p_outgoing, q_incoming, adjacency_matrix, Ws, bs, ou
                 in_=node_grouped[side][:, c * K_PASS * PACK:(c + 1) * K_PASS * PACK],
             )
 
-        def regroup_adjacency(c, half):
-            j0 = half * HALF
-            dst = adj_grouped[0][:, (c * NODES + j0) * PACK:(c * NODES + j0 + HALF) * PACK]
-            nc.scalar.copy(
-                out=dst.rearrange("p (b i t) -> p b t i", i=4, t=PACK),
-                in_=a_rows[:, c, :, j0:j0 + HALF].rearrange("p t (b i) -> p b t i", i=4),
-            )
+        def regroup_adjacency(c, j0, j1, on_gpsimd=False):
+            dst = adj_grouped[0][:, (c * NODES + j0) * PACK:(c * NODES + j1) * PACK]
+            out = dst.rearrange("p (b i t) -> p b t i", i=4, t=PACK)
+            in_ = a_rows[:, c, :, j0:j1].rearrange("p t (b i) -> p b t i", i=4)
+            if on_gpsimd:
+                nc.gpsimd.tensor_scalar(out=out, in0=in_, scalar1=1.0, scalar2=0.0, op0=ALU.mult, op1=ALU.add)
+            else:
+                nc.scalar.copy(out=out, in_=in_)
 
         def transpose_adjacency(g, half):
             for pair in range(2 * half, 2 * half + 2):
@@ -176,40 +177,49 @@ def tile_gglr_pa_kernel(tc, p_outgoing, q_incoming, adjacency_matrix, Ws, bs, ou
         recip_big = [keep.tile([P, BANKS], F32, name="recip_big%d" % s) for s in range(2)]
         d_in = keep.tile([P, BANKS], F32)
 
-        def scaled_reciprocals(side):
-            nc.vector.tensor_scalar_mul(out=recip_small[side][:], in0=recip[side][:], scalar1=SLOPE)
-            nc.vector.tensor_scalar_mul(out=recip_big[side][:], in0=recip[side][:], scalar1=1.0 - SLOPE)
+        def scaled_reciprocals(side, cols):
+            nc.vector.tensor_scalar_mul(out=recip_small[side][:, cols], in0=recip[side][:, cols], scalar1=SLOPE)
+            nc.vector.tensor_scalar_mul(out=recip_big[side][:, cols], in0=recip[side][:, cols], scalar1=1.0 - SLOPE)
 
-        def degree_out():
-            sums = psum.tile([P, BANKS, 64], F32, tag="bank")
-            for m in range(BANKS):
+        d_out_sums = psum.tile([P, BANKS, 64], F32, tag="sums", bufs=1)
+
+        def degree_out(m0, m1):
+            for m in range(m0, m1):
                 for r in range(BANKS):
                     nc.tensor.matmul(
-                        out=sums[:, m, :],
+                        out=d_out_sums[:, m, :],
                         lhsT=a_rows[:, r // PACK, r % PACK, m * P:(m + 1) * P],
                         rhs=ones[:, 0:64],
                         start=(r == 0),
                         stop=(r == BANKS - 1),
                     )
-            nc.vector.reciprocal(out=recip[0][:], in_=sums[:, :, 0])
-            scaled_reciprocals(0)
 
-        def degree_in(c):
-            folded = psum.tile([P, PACK, P], F32, tag="bank")
-            for t in range(PACK):
+        def degree_out_reciprocals():
+            nc.vector.reciprocal(out=recip[0][:], in_=d_out_sums[:, :, 0])
+            scaled_reciprocals(0, slice(0, BANKS))
+
+        def degree_in(m0):
+            folded = psum.tile([P, 2, P], F32, tag="bank")
+            for i in range(2):
                 for s in range(NODES // P):
                     nc.tensor.matmul(
-                        out=folded[:, t, :],
+                        out=folded[:, i, :],
                         lhsT=ident_bf16[:],
-                        rhs=a_rows[:, c, t, s * P:(s + 1) * P],
+                        rhs=a_rows[:, m0 // PACK, m0 % PACK + i, s * P:(s + 1) * P],
                         start=(s == 0),
                         stop=(s == NODES // P - 1),
                     )
-            nc.vector.tensor_reduce(out=d_in[:, c * PACK:(c + 1) * PACK], in_=folded[:], axis=AX.X, op=ALU.add)
+            return lambda: nc.vector.tensor_reduce(out=d_in[:, m0:m0 + 2], in_=folded[:], axis=AX.X, op=ALU.add)
+
+        def degree_in_scalar(m):
+            passed = work.tile([P, NODES], BF16, tag="passed", bufs=2)
+            nc.scalar.activation(
+                out=passed[:], in_=a_rows[:, m // PACK, m % PACK, :], func=ACT.Copy, accum_out=d_in[:, m:m + 1]
+            )
 
         def degree_in_reciprocals():
             nc.vector.reciprocal(out=recip[1][:], in_=d_in[:])
-            scaled_reciprocals(1)
+            scaled_reciprocals(1, slice(0, BANKS))
 
         w_grouped = {}
         w_codes = {}
@@ -290,29 +300,33 @@ def tile_gglr_pa_kernel(tc, p_outgoing, q_incoming, adjacency_matrix, Ws, bs, ou
         transpose_nodes(0, 1, share_with_vector=True)
         spread_bias()
         quantise_nodes(0, 1)
-        for n in range(0, 2):
+        regroup_adjacency(0, 0, 512)
+        regroup_adjacency(0, 512, 768, on_gpsimd=True)
+        regroup_adjacency(0, 768, 1024, on_gpsimd=True)
+        regroup_adjacency(1, 0, 256, on_gpsimd=True)
+        regroup_adjacency(1, 256, 512, on_gpsimd=True)
+        for n in range(BANKS):
             stage1_bank(n)
-        regroup_adjacency(0, 0)
-        for n in range(2, 5):
-            stage1_bank(n)
-        regroup_adjacency(0, 1)
-        for n in range(5, BANKS):
-            stage1_bank(n)
-        quantise_stage1(0, 0)
-        degree_in(0)
-        quantise_stage1(0, 1)
-        regroup_adjacency(1, 0)
-        degree_out()
-        regroup_adjacency(1, 1)
-        for c in range(PASSES):
-            for half in range(2):
-                quantise_adjacency(0, c, half)
         transpose_weights(1)
-        quantise_weights(1)
+        degree_in_scalar(0)
+        degree_in_scalar(1)
+        degree_out(0, 4)
         transpose_weights(2)
-        degree_in(1)
+        quantise_weights(1)
+        quantise_stage1(0, 0)
+        regroup_adjacency(1, 512, 1024)
+        quantise_stage1(0, 1)
+        for n in range(BANKS, BANKS + 4):
+            stage1_bank(n)
+        degree_out(4, 8)
+        quantise_adjacency(0, 0, 0)
+        quantise_adjacency(0, 1, 0)
         quantise_weights(2)
-        degree_in_reciprocals()
+        quantise_stage1(1, 0)
+        transpose_nodes(1, 0)
+        degree_out_reciprocals()
+        quantise_adjacency(0, 0, 1)
+        quantise_adjacency(0, 1, 1)
 
         def stage1_block(b):
             for n in range(b * BLOCK, (b + 1) * BLOCK):
@@ -322,7 +336,6 @@ def tile_gglr_pa_kernel(tc, p_outgoing, q_incoming, adjacency_matrix, Ws, bs, ou
             quantise_stage1(b // PASSES, b % PASSES)
 
         later_transposes = [
-            lambda: transpose_nodes(1, 0),
             lambda: transpose_nodes(1, 1),
             lambda: transpose_adjacency(0, 0),
             lambda: transpose_adjacency(1, 0),
@@ -338,21 +351,25 @@ def tile_gglr_pa_kernel(tc, p_outgoing, q_incoming, adjacency_matrix, Ws, bs, ou
             lambda: quantise_adjacency(1, 1, 1),
         ]
 
-        stage1_block(LEAD_BLOCKS - 1)
-        later_transposes[0]()
-        quantise_block(LEAD_BLOCKS - 1)
+        pending = []
         for r in range(ROUNDS):
             first = r * BLOCK
             ahead = r + LEAD_BLOCKS
             stage2_bank(first)
             stage2_bank(first + 1)
+            while pending:
+                pending.pop()()
             if ahead < ROUNDS:
                 stage1_block(ahead)
             stage2_bank(first + 2)
             stage2_bank(first + 3)
-            if r + 1 < len(later_transposes):
-                later_transposes[r + 1]()
+            if r < len(later_transposes):
+                later_transposes[r]()
+            if 1 <= r <= 3:
+                pending.append(degree_in(2 * r))
             if r < len(later_quantises):
                 later_quantises[r]()
+            if r == 5:
+                degree_in_reciprocals()
             if ahead < ROUNDS:
                 quantise_block(ahead)

@@ -39,7 +39,7 @@ def tile_gglr_pa_kernel(tc, p_outgoing, q_incoming, adjacency_matrix, Ws, bs, ou
         keep = ctx.enter_context(tc.tile_pool(name="keep", bufs=1))
         wpool = ctx.enter_context(tc.tile_pool(name="wpool", bufs=2))
         work = ctx.enter_context(tc.tile_pool(name="work", bufs=4))
-        outp = ctx.enter_context(tc.tile_pool(name="outp", bufs=6))
+        outp = ctx.enter_context(tc.tile_pool(name="outp", bufs=10))
         psum = ctx.enter_context(tc.psum_pool(name="psum", bufs=7))
         ctx.enter_context(tc.manual_schedule())
 
@@ -166,11 +166,17 @@ def tile_gglr_pa_kernel(tc, p_outgoing, q_incoming, adjacency_matrix, Ws, bs, ou
             )
 
         def spread_bias():
-            for k in range(LAYERS):
-                feats = slice(k * D, (k + 1) * D)
-                bank = psum.tile([P, D], F32, tag="bank")
-                nc.tensor.matmul(out=bank[:], lhsT=ones[:], rhs=bias_row[:, feats], start=True, stop=True)
-                nc.scalar.copy(out=bias[:, feats], in_=bank[:])
+            for k0, k1 in ((0, 1), (1, 3)):
+                bank = psum.tile([P, 2 * D], BF16, tag="bank")
+                for k in range(k0, k1):
+                    nc.tensor.matmul(
+                        out=bank[:, (k - k0) * D:(k - k0 + 1) * D],
+                        lhsT=ones[:],
+                        rhs=bias_row[:, k * D:(k + 1) * D],
+                        start=True,
+                        stop=True,
+                    )
+                nc.scalar.copy(out=bias[:, k0 * D:k1 * D], in_=bank[:, 0:(k1 - k0) * D])
 
         recip = [keep.tile([P, BANKS], F32, name="recip%d" % s) for s in range(2)]
         recip_small = [keep.tile([P, BANKS], F32, name="recip_small%d" % s) for s in range(2)]
@@ -307,6 +313,7 @@ def tile_gglr_pa_kernel(tc, p_outgoing, q_incoming, adjacency_matrix, Ws, bs, ou
         regroup_adjacency(1, 256, 512, on_gpsimd=True)
         for n in range(BANKS):
             stage1_bank(n)
+        pending = [degree_in(2)]
         transpose_weights(1)
         degree_in_scalar(0)
         degree_in_scalar(1)
@@ -314,6 +321,8 @@ def tile_gglr_pa_kernel(tc, p_outgoing, q_incoming, adjacency_matrix, Ws, bs, ou
         transpose_weights(2)
         quantise_weights(1)
         quantise_stage1(0, 0)
+        while pending:
+            pending.pop()()
         regroup_adjacency(1, 512, 1024)
         quantise_stage1(0, 1)
         for n in range(BANKS, BANKS + 4):
@@ -321,10 +330,12 @@ def tile_gglr_pa_kernel(tc, p_outgoing, q_incoming, adjacency_matrix, Ws, bs, ou
         degree_out(4, 8)
         quantise_adjacency(0, 0, 0)
         quantise_adjacency(0, 1, 0)
+        degree_out_reciprocals()
         quantise_weights(2)
+
         quantise_stage1(1, 0)
         transpose_nodes(1, 0)
-        degree_out_reciprocals()
+
         quantise_adjacency(0, 0, 1)
         quantise_adjacency(0, 1, 1)
 
@@ -365,8 +376,8 @@ def tile_gglr_pa_kernel(tc, p_outgoing, q_incoming, adjacency_matrix, Ws, bs, ou
             stage2_bank(first + 3)
             if r < len(later_transposes):
                 later_transposes[r]()
-            if 1 <= r <= 3:
-                pending.append(degree_in(2 * r))
+            if r in (2, 4):
+                pending.append(degree_in(2 + r))
             if r < len(later_quantises):
                 later_quantises[r]()
             if r == 5:

@@ -40,7 +40,7 @@ def tile_gglr_pa_kernel(tc, p_outgoing, q_incoming, adjacency_matrix, Ws, bs, ou
         wpool = ctx.enter_context(tc.tile_pool(name="wpool", bufs=2))
         work = ctx.enter_context(tc.tile_pool(name="work", bufs=4))
         outp = ctx.enter_context(tc.tile_pool(name="outp", bufs=10))
-        psum = ctx.enter_context(tc.psum_pool(name="psum", bufs=7))
+        psum = ctx.enter_context(tc.psum_pool(name="psum", bufs=8))
         ctx.enter_context(tc.manual_schedule())
 
         ident_f32 = keep.tile([P, P], F32)
@@ -187,22 +187,24 @@ def tile_gglr_pa_kernel(tc, p_outgoing, q_incoming, adjacency_matrix, Ws, bs, ou
             nc.vector.tensor_scalar_mul(out=recip_small[side][:, cols], in0=recip[side][:, cols], scalar1=SLOPE)
             nc.vector.tensor_scalar_mul(out=recip_big[side][:, cols], in0=recip[side][:, cols], scalar1=1.0 - SLOPE)
 
-        d_out_sums = psum.tile([P, BANKS, 64], F32, tag="sums", bufs=1)
+        d_out_sums = {}
 
-        def degree_out(m0, m1):
-            for m in range(m0, m1):
+        def degree_out(half):
+            d_out_sums[half] = psum.tile([P, PACK, 64], F32, tag="bank", name="d_out_sums%d" % half)
+            for m in range(half * PACK, (half + 1) * PACK):
                 for r in range(BANKS):
                     nc.tensor.matmul(
-                        out=d_out_sums[:, m, :],
+                        out=d_out_sums[half][:, m % PACK, :],
                         lhsT=a_rows[:, r // PACK, r % PACK, m * P:(m + 1) * P],
                         rhs=ones[:, 0:64],
                         start=(r == 0),
                         stop=(r == BANKS - 1),
                     )
 
-        def degree_out_reciprocals():
-            nc.vector.reciprocal(out=recip[0][:], in_=d_out_sums[:, :, 0])
-            scaled_reciprocals(0, slice(0, BANKS))
+        def degree_out_reciprocals(half):
+            cols = slice(half * PACK, (half + 1) * PACK)
+            nc.vector.reciprocal(out=recip[0][:, cols], in_=d_out_sums[half][:, :, 0])
+            scaled_reciprocals(0, cols)
 
         def degree_in(m0):
             folded = psum.tile([P, 2, P], F32, tag="bank")
@@ -309,33 +311,31 @@ def tile_gglr_pa_kernel(tc, p_outgoing, q_incoming, adjacency_matrix, Ws, bs, ou
         regroup_adjacency(0, 0, 512)
         regroup_adjacency(0, 512, 768, on_gpsimd=True)
         regroup_adjacency(0, 768, 1024, on_gpsimd=True)
-        regroup_adjacency(1, 0, 256, on_gpsimd=True)
-        regroup_adjacency(1, 256, 512, on_gpsimd=True)
+        regroup_adjacency(1, 0, 512)
         for n in range(BANKS):
             stage1_bank(n)
         pending = [degree_in(2)]
         transpose_weights(1)
         degree_in_scalar(0)
         degree_in_scalar(1)
-        degree_out(0, 4)
+        degree_out(0)
         transpose_weights(2)
         quantise_weights(1)
         quantise_stage1(0, 0)
+        degree_out_reciprocals(0)
         while pending:
             pending.pop()()
         regroup_adjacency(1, 512, 1024)
         quantise_stage1(0, 1)
         for n in range(BANKS, BANKS + 4):
             stage1_bank(n)
-        degree_out(4, 8)
+        degree_out(1)
         quantise_adjacency(0, 0, 0)
         quantise_adjacency(0, 1, 0)
-        degree_out_reciprocals()
+        degree_out_reciprocals(1)
         quantise_weights(2)
-
         quantise_stage1(1, 0)
         transpose_nodes(1, 0)
-
         quantise_adjacency(0, 0, 1)
         quantise_adjacency(0, 1, 1)
 
@@ -366,21 +366,27 @@ def tile_gglr_pa_kernel(tc, p_outgoing, q_incoming, adjacency_matrix, Ws, bs, ou
         for r in range(ROUNDS):
             first = r * BLOCK
             ahead = r + LEAD_BLOCKS
-            stage2_bank(first)
-            stage2_bank(first + 1)
+            stage2_bank(first + 0)
             while pending:
                 pending.pop()()
             if ahead < ROUNDS:
-                stage1_block(ahead)
+                stage1_bank(ahead * BLOCK + 0)
+            stage2_bank(first + 1)
+            if ahead < ROUNDS:
+                stage1_bank(ahead * BLOCK + 1)
+            if ahead < ROUNDS:
+                stage1_bank(ahead * BLOCK + 2)
+            if ahead < ROUNDS:
+                stage1_bank(ahead * BLOCK + 3)
             stage2_bank(first + 2)
-            stage2_bank(first + 3)
-            if r < len(later_transposes):
-                later_transposes[r]()
-            if r in (2, 4):
-                pending.append(degree_in(2 + r))
             if r < len(later_quantises):
                 later_quantises[r]()
             if r == 5:
                 degree_in_reciprocals()
+            if r < len(later_transposes):
+                later_transposes[r]()
+            stage2_bank(first + 3)
             if ahead < ROUNDS:
                 quantise_block(ahead)
+            if r in (2, 4):
+                pending.append(degree_in(2 + r))

@@ -80,10 +80,10 @@ def tile_gglr_pa_kernel(tc, p_outgoing, q_incoming, adjacency_matrix, Ws, bs, ou
             )
 
         load_ws(0, 0, 2)
-        nc.sync.dma_start(out=bias_row[0:1, :], in_=bs.rearrange("(o k) d -> o (k d)", o=1))
         load_ws(0, 2, 4)
         load_p(0, 0, 2)
         load_p(0, 2, 4)
+        nc.sync.dma_start(out=bias_row[0:1, :], in_=bs.rearrange("(o k) d -> o (k d)", o=1))
         load_p(1, 0, 4)
         load_a(0)
         load_a(1)
@@ -320,8 +320,8 @@ def tile_gglr_pa_kernel(tc, p_outgoing, q_incoming, adjacency_matrix, Ws, bs, ou
         degree_in_scalar(1)
         degree_out(0)
         transpose_weights(2)
-        quantise_weights(1)
         quantise_stage1(0, 0)
+        quantise_weights(1)
         degree_out_reciprocals(0)
         while pending:
             pending.pop()()

@@ -183,9 +183,9 @@ def tile_gglr_pa_kernel(tc, p_outgoing, q_incoming, adjacency_matrix, Ws, bs, ou
         recip_big = [keep.tile([P, BANKS], F32, name="recip_big%d" % s) for s in range(2)]
         d_in = keep.tile([P, BANKS], F32)
 
-        def scaled_reciprocals(side, cols):
-            nc.vector.tensor_scalar_mul(out=recip_small[side][:, cols], in0=recip[side][:, cols], scalar1=SLOPE)
-            nc.vector.tensor_scalar_mul(out=recip_big[side][:, cols], in0=recip[side][:, cols], scalar1=1.0 - SLOPE)
+        def scaled_reciprocals(side):
+            nc.vector.tensor_scalar_mul(out=recip_small[side][:], in0=recip[side][:], scalar1=SLOPE)
+            nc.vector.tensor_scalar_mul(out=recip_big[side][:], in0=recip[side][:], scalar1=1.0 - SLOPE)
 
         d_out_sums = {}
 
@@ -204,7 +204,6 @@ def tile_gglr_pa_kernel(tc, p_outgoing, q_incoming, adjacency_matrix, Ws, bs, ou
         def degree_out_reciprocals(half):
             cols = slice(half * PACK, (half + 1) * PACK)
             nc.vector.reciprocal(out=recip[0][:, cols], in_=d_out_sums[half][:, :, 0])
-            scaled_reciprocals(0, cols)
 
         def degree_in(m0):
             folded = psum.tile([P, 2, P], F32, tag="bank")
@@ -227,7 +226,7 @@ def tile_gglr_pa_kernel(tc, p_outgoing, q_incoming, adjacency_matrix, Ws, bs, ou
 
         def degree_in_reciprocals():
             nc.vector.reciprocal(out=recip[1][:], in_=d_in[:])
-            scaled_reciprocals(1, slice(0, BANKS))
+            scaled_reciprocals(1)
 
         w_grouped = {}
         w_codes = {}
@@ -302,38 +301,40 @@ def tile_gglr_pa_kernel(tc, p_outgoing, q_incoming, adjacency_matrix, Ws, bs, ou
                 nc.sync.dma_start(out=q_out[k, m // PACK, m % PACK], in_=result[:])
 
         transpose_weights(0, share_with_vector=True)
-        transpose_nodes(0, 0, share_with_vector=True)
         quantise_weights(0)
+        transpose_nodes(0, 0, share_with_vector=True)
         quantise_nodes(0, 0)
-        transpose_nodes(0, 1, share_with_vector=True)
+        transpose_nodes(0, 1)
         spread_bias()
         quantise_nodes(0, 1)
         regroup_adjacency(0, 0, 512)
         regroup_adjacency(0, 512, 768, on_gpsimd=True)
         regroup_adjacency(0, 768, 1024, on_gpsimd=True)
-        regroup_adjacency(1, 0, 512)
+        regroup_adjacency(1, 512, 768, on_gpsimd=True)
+        regroup_adjacency(1, 768, 1024, on_gpsimd=True)
         for n in range(BANKS):
             stage1_bank(n)
-        pending = [degree_in(2)]
         transpose_weights(1)
+        regroup_adjacency(1, 0, 512)
+        pending = [degree_in(2)]
         degree_in_scalar(0)
         degree_in_scalar(1)
         degree_out(0)
         transpose_weights(2)
         quantise_stage1(0, 0)
+        quantise_adjacency(0, 0, 0)
         quantise_weights(1)
         degree_out_reciprocals(0)
         while pending:
             pending.pop()()
-        regroup_adjacency(1, 512, 1024)
         quantise_stage1(0, 1)
         for n in range(BANKS, BANKS + 4):
             stage1_bank(n)
         degree_out(1)
-        quantise_adjacency(0, 0, 0)
         quantise_adjacency(0, 1, 0)
         degree_out_reciprocals(1)
         quantise_weights(2)
+        scaled_reciprocals(0)
         quantise_stage1(1, 0)
         transpose_nodes(1, 0)
         quantise_adjacency(0, 0, 1)

from contextlib import ExitStack

import concourse.mybir as mybir
from concourse.masks import make_identity

FP8X4 = mybir.dt.float8_e4m3fn_x4
BF16 = mybir.dt.bfloat16
F32 = mybir.dt.float32
U32 = mybir.dt.uint32
U8 = mybir.dt.uint8
I32 = mybir.dt.int32
ALU = mybir.AluOpType
ACT = mybir.ActivationFunctionType
AX = mybir.AxisListType

P = 128
PACK = 4
K_PASS = P * PACK
NODES = 1024
D = 512
LAYERS = 3
PASSES = NODES // K_PASS
HALF = 512
SLOPE = 0.01
FLOPS = 2 * 2 * LAYERS * NODES * D * (D + NODES)

UNITS = [(0, 0), (1, 0), (2, 0), (0, 1), (1, 1), (2, 1)]
BANKS = 8
N_BANKS = BANKS * len(UNITS)
BLOCK = 4
ROUNDS = N_BANKS // BLOCK
LEAD_BLOCKS = 3
GPSIMD_ROUNDS = 9


def tile_gglr_pa_kernel(tc, p_outgoing, q_incoming, adjacency_matrix, Ws, bs, out_0, out_1):
    nc = tc.nc
    with ExitStack() as ctx:
        keep = ctx.enter_context(tc.tile_pool(name="keep", bufs=1))
        wpool = ctx.enter_context(tc.tile_pool(name="wpool", bufs=2))
        work = ctx.enter_context(tc.tile_pool(name="work", bufs=4))
        outp = ctx.enter_context(tc.tile_pool(name="outp", bufs=10))
        psum = ctx.enter_context(tc.psum_pool(name="psum", bufs=8))
        ctx.enter_context(tc.manual_schedule())

        ident_f32 = keep.tile([P, P], F32)
        make_identity(nc, ident_f32[:])
        ident_bf16 = keep.tile([P, P], BF16)
        make_identity(nc, ident_bf16[:])
        bias_row = keep.tile([P, LAYERS * D], BF16)
        nc.vector.memset(bias_row[:].bitcast(I32), 0)
        ones = keep.tile([P, P], BF16)
        nc.vector.memset(ones[:], 1.0)
        bias = keep.tile([P, LAYERS * D], BF16)

        ws_rows = keep.tile([P, LAYERS, PACK, D], BF16)
        p_rows = keep.tile([P, PASSES, PACK, D], BF16)
        q_rows = keep.tile([P, PASSES, PACK, D], BF16)
        a_rows = keep.tile([P, PASSES, PACK, NODES], BF16)

        def load_ws(k, o0, o1):
            nc.sync.dma_start(
                out=ws_rows[:, k, o0:o1], in_=Ws[k, o0 * P:o1 * P, :].rearrange("(o r) i -> r o i", r=P)
            )

        def load_p(c, t0, t1):
            rows = p_outgoing[c * K_PASS:(c + 1) * K_PASS, :].rearrange("(p t) d -> p t d", t=PACK)
            nc.sync.dma_start(out=p_rows[:, c, t0:t1], in_=rows[:, t0:t1, :])

        def load_q(g):
            nc.sync.dma_start(
                out=q_rows[:, g].rearrange("p (u e) d -> p u e d", u=2),
                in_=q_incoming[g * K_PASS:(g + 1) * K_PASS, :].rearrange("(u p e) d -> p u e d", u=2, e=2),
            )

        def load_a(c):
            nc.sync.dma_start(
                out=a_rows[:, c],
                in_=adjacency_matrix[c * K_PASS:(c + 1) * K_PASS, :].rearrange("(p t) j -> p t j", t=PACK),
            )

        load_ws(0, 0, 2)
        load_ws(0, 2, 4)
        load_p(0, 0, 2)
        load_p(0, 2, 4)
        nc.sync.dma_start(out=bias_row[0:1, :], in_=bs.rearrange("(o k) d -> o (k d)", o=1))
        load_p(1, 0, 4)
        load_a(0)
        load_a(1)
        load_ws(1, 0, 4)
        load_ws(2, 0, 4)
        load_q(0)
        load_q(1)

        ws_grouped = keep.tile([P, LAYERS * D * PACK], BF16, align_bytes=64)
        ws_codes = keep.tile([P, LAYERS, D], U32, align_bytes=64)
        ws_scales = keep.tile([P, LAYERS, D], U8, align_bytes=64)
        node_grouped = [keep.tile([P, NODES * PACK], BF16, align_bytes=64, name="node_grouped%d" % s) for s in range(2)]
        node_codes = [keep.tile([P, NODES], U32, align_bytes=64, name="node_codes%d" % s) for s in range(2)]
        node_scales = [keep.tile([P, NODES], U8, align_bytes=64, name="node_scales%d" % s) for s in range(2)]
        adj_grouped = [keep.tile([P, PASSES * NODES * PACK], BF16, align_bytes=64, name="adj_grouped%d" % s) for s in range(2)]
        adj_codes = [keep.tile([P, PASSES, NODES], U32, align_bytes=64, name="adj_codes%d" % s) for s in range(2)]
        adj_scales = [keep.tile([P, PASSES, NODES], U8, align_bytes=64, name="adj_scales%d" % s) for s in range(2)]

        def transpose_two(tiles, grouped, col0, on_vector=False):
            bank = psum.tile([P, 2, 2 * P], F32, tag="bank")
            for h in range(2):
                words = tiles[h].bitcast(F32)
                for u in range(2):
                    nc.tensor.transpose(bank[:, u, h * P:(h + 1) * P], words[:, u * P:(u + 1) * P], ident_f32[:])
            dst = grouped[:].bitcast(F32)[:, col0 * 2:(col0 + 2 * P) * 2].rearrange("p (r u) -> p r u", u=2)
            src = bank[:].rearrange("p u r -> p r u")
            if on_vector:
                nc.vector.tensor_copy(out=dst, in_=src)
            else:
                nc.scalar.copy(out=dst, in_=src)

        def transpose_weights(k, share_with_vector=False):
            for h in range(2):
                tiles = [ws_rows[:, k, 2 * h + i, :] for i in range(2)]
                transpose_two(tiles, ws_grouped, k * D + h * 2 * P, on_vector=share_with_vector and h == 1)

        def quantise_weights(k):
            nc.vector.quantize_mx(
                out=ws_codes[:, k, :].bitcast(FP8X4),
                scales=ws_scales[:, k, :],
                in_=ws_grouped[:, k * D * PACK:(k + 1) * D * PACK],
            )

        def transpose_nodes(side, c, share_with_vector=False):
            rows = p_rows if side == 0 else q_rows
            for h in range(2):
                tiles = [rows[:, c, 2 * h + i, :] for i in range(2)]
                transpose_two(tiles, node_grouped[side], c * K_PASS + h * 2 * P, on_vector=share_with_vector and h == 1)

        def quantise_nodes(side, c):
            cols = slice(c * K_PASS, (c + 1) * K_PASS)
            nc.vector.quantize_mx(
                out=node_codes[side][:, cols].bitcast(FP8X4),
                scales=node_scales[side][:, cols],
                in_=node_grouped[side][:, c * K_PASS * PACK:(c + 1) * K_PASS * PACK],
            )

        def regroup_adjacency(c, j0, j1, on_gpsimd=False):
            dst = adj_grouped[0][:, (c * NODES + j0) * PACK:(c * NODES + j1) * PACK]
            out = dst.rearrange("p (b i t) -> p b t i", i=4, t=PACK)
            in_ = a_rows[:, c, :, j0:j1].rearrange("p t (b i) -> p b t i", i=4)
            if on_gpsimd:
                nc.gpsimd.tensor_scalar(out=out, in0=in_, scalar1=1.0, scalar2=0.0, op0=ALU.mult, op1=ALU.add)
            else:
                nc.scalar.copy(out=out, in_=in_)

        def transpose_adjacency(g, half):
            for pair in range(2 * half, 2 * half + 2):
                tiles = []
                for m in range(2 * pair, 2 * pair + 2):
                    tiles.append(a_rows[:, m // PACK, m % PACK, g * K_PASS:(g + 1) * K_PASS])
                transpose_two(tiles, adj_grouped[1], g * NODES + pair * 2 * P)

        def quantise_adjacency(side, c, half):
            j0 = half * HALF
            nc.vector.quantize_mx(
                out=adj_codes[side][:, c, j0:j0 + HALF].bitcast(FP8X4),
                scales=adj_scales[side][:, c, j0:j0 + HALF],
                in_=adj_grouped[side][:, (c * NODES + j0) * PACK:(c * NODES + j0 + HALF) * PACK],
            )

        def spread_bias():
            for k0, k1 in ((0, 1), (1, 3)):
                bank = psum.tile([P, 2 * D], BF16, tag="bank")
                for k in range(k0, k1):
                    nc.tensor.matmul(
                        out=bank[:, (k - k0) * D:(k - k0 + 1) * D],
                        lhsT=ones[:],
                        rhs=bias_row[:, k * D:(k + 1) * D],
                        start=True,
                        stop=True,
                    )
                nc.scalar.copy(out=bias[:, k0 * D:k1 * D], in_=bank[:, 0:(k1 - k0) * D])

        recip = [keep.tile([P, BANKS], F32, name="recip%d" % s) for s in range(2)]
        recip_small = [keep.tile([P, BANKS], F32, name="recip_small%d" % s) for s in range(2)]
        recip_big = [keep.tile([P, BANKS], F32, name="recip_big%d" % s) for s in range(2)]
        d_in = keep.tile([P, BANKS], F32)

        def scaled_reciprocals(side):
            nc.vector.tensor_scalar_mul(out=recip_small[side][:], in0=recip[side][:], scalar1=SLOPE)
            nc.vector.tensor_scalar_mul(out=recip_big[side][:], in0=recip[side][:], scalar1=1.0 - SLOPE)

        d_out_sums = {}

        def degree_out(half):
            d_out_sums[half] = psum.tile([P, PACK, 64], F32, tag="bank", name="d_out_sums%d" % half)
            for m in range(half * PACK, (half + 1) * PACK):
                for r in range(BANKS):
                    nc.tensor.matmul(
                        out=d_out_sums[half][:, m % PACK, :],
                        lhsT=a_rows[:, r // PACK, r % PACK, m * P:(m + 1) * P],
                        rhs=ones[:, 0:64],
                        start=(r == 0),
                        stop=(r == BANKS - 1),
                    )

        def degree_out_reciprocals(half):
            cols = slice(half * PACK, (half + 1) * PACK)
            nc.vector.reciprocal(out=recip[0][:, cols], in_=d_out_sums[half][:, :, 0])

        def degree_in(m0):
            folded = psum.tile([P, 2, P], F32, tag="bank")
            for i in range(2):
                for s in range(NODES // P):
                    nc.tensor.matmul(
                        out=folded[:, i, :],
                        lhsT=ident_bf16[:],
                        rhs=a_rows[:, m0 // PACK, m0 % PACK + i, s * P:(s + 1) * P],
                        start=(s == 0),
                        stop=(s == NODES // P - 1),
                    )
            return lambda: nc.vector.tensor_reduce(out=d_in[:, m0:m0 + 2], in_=folded[:], axis=AX.X, op=ALU.add)

        def degree_in_scalar(m):
            passed = work.tile([P, NODES], BF16, tag="passed", bufs=2)
            nc.scalar.activation(
                out=passed[:], in_=a_rows[:, m // PACK, m % PACK, :], func=ACT.Copy, accum_out=d_in[:, m:m + 1]
            )

        def degree_in_reciprocals():
            nc.vector.reciprocal(out=recip[1][:], in_=d_in[:])
            scaled_reciprocals(1)

        w_grouped = {}
        w_codes = {}
        w_scales = {}

        def stage1_bank(n):
            unit, b = n // BANKS, n % BANKS
            k, side = UNITS[unit]
            c, f = b // PACK, b % PACK
            if b == 0:
                w_grouped[unit] = wpool.tile([P, PASSES, D, PACK], BF16, tag="w_grouped", align_bytes=64, name="w_grouped%d" % unit)
                w_codes[unit] = wpool.tile([P, PASSES, D], U32, tag="w_codes", bufs=4, align_bytes=64, name="w_codes%d" % unit)
                w_scales[unit] = wpool.tile([P, PASSES, D], U8, tag="w_scales", bufs=4, align_bytes=64, name="w_scales%d" % unit)
            feats = slice(f * P, (f + 1) * P)
            bank = psum.tile([P, PACK, P], F32, tag="bank")
            for t in range(PACK):
                nodes = slice((c * PACK + t) * P, (c * PACK + t + 1) * P)
                nc.tensor.matmul_mx(
                    out=bank[:, t, :],
                    lhsT=node_codes[side][:, nodes].bitcast(FP8X4),
                    lhsT_scale=node_scales[side][:, nodes],
                    rhs=ws_codes[:, k, feats].bitcast(FP8X4),
                    rhs_scale=ws_scales[:, k, feats],
                    start=True,
                    stop=True,
                )
            nc.vector.tensor_tensor(
                out=w_grouped[unit][:, c, feats, :],
                in0=bank[:].rearrange("p t d -> p d t"),
                in1=bias[:, k * D + f * P:k * D + (f + 1) * P].unsqueeze(2).to_broadcast([P, P, PACK]),
                op=ALU.add,
            )

        def quantise_stage1(unit, c):
            nc.vector.quantize_mx(
                out=w_codes[unit][:, c, :].bitcast(FP8X4),
                scales=w_scales[unit][:, c, :],
                in_=w_grouped[unit][:, c].rearrange("p d t -> p (d t)"),
            )

        q_out = out_1.rearrange("k (c p t) d -> k c t p d", c=PASSES, t=PACK)

        def stage2_bank(n):
            unit, m = n // BANKS, n % BANKS
            k, side = UNITS[unit]
            nodes = slice(m * P, (m + 1) * P)
            bank = psum.tile([P, D], F32, tag="bank")
            for c in range(PASSES):
                nc.tensor.matmul_mx(
                    out=bank[:],
                    lhsT=adj_codes[side][:, c, nodes].bitcast(FP8X4),
                    lhsT_scale=adj_scales[side][:, c, nodes],
                    rhs=w_codes[unit][:, c, :].bitcast(FP8X4),
                    rhs_scale=w_scales[unit][:, c, :],
                    start=(c == 0),
                    stop=(c == PASSES - 1),
                )
            result = outp.tile([P, D], F32, tag="result")
            small = work.tile([P, D], F32, tag="small")
            nc.scalar.activation(out=small[:], in_=bank[:], func=ACT.Copy, scale=recip_small[side][:, m:m + 1])
            if n % BLOCK < 2 and n // BLOCK < GPSIMD_ROUNDS:
                big = work.tile([P, D], F32, tag="big")
                nc.scalar.activation(out=big[:], in_=bank[:], func=ACT.Relu, scale=recip_big[side][:, m:m + 1])
                nc.gpsimd.tensor_tensor(out=result[:], in0=big[:], in1=small[:], op=ALU.add)
            else:
                nc.vector.scalar_tensor_tensor(
                    out=result[:], in0=bank[:], scalar=recip[side][:, m:m + 1], in1=small[:], op0=ALU.mult, op1=ALU.max
                )
            if side == 0:
                nc.sync.dma_start(out=out_0[k, nodes, :], in_=result[:])
            else:
                nc.sync.dma_start(out=q_out[k, m // PACK, m % PACK], in_=result[:])

        transpose_weights(0, share_with_vector=True)
        quantise_weights(0)
        transpose_nodes(0, 0, share_with_vector=True)
        quantise_nodes(0, 0)
        transpose_nodes(0, 1)
        spread_bias()
        quantise_nodes(0, 1)
        regroup_adjacency(0, 0, 512)
        regroup_adjacency(0, 512, 768, on_gpsimd=True)
        regroup_adjacency(0, 768, 1024, on_gpsimd=True)
        regroup_adjacency(1, 512, 768, on_gpsimd=True)
        regroup_adjacency(1, 768, 1024, on_gpsimd=True)
        for n in range(BANKS):
            stage1_bank(n)
        transpose_weights(1)
        regroup_adjacency(1, 0, 512)
        pending = [degree_in(2)]
        degree_in_scalar(0)
        degree_in_scalar(1)
        degree_out(0)
        transpose_weights(2)
        quantise_stage1(0, 0)
        quantise_adjacency(0, 0, 0)
        quantise_weights(1)
        degree_out_reciprocals(0)
        while pending:
            pending.pop()()
        quantise_stage1(0, 1)
        for n in range(BANKS, BANKS + 4):
            stage1_bank(n)
        degree_out(1)
        quantise_adjacency(0, 1, 0)
        degree_out_reciprocals(1)
        quantise_weights(2)
        scaled_reciprocals(0)
        quantise_stage1(1, 0)
        transpose_nodes(1, 0)
        quantise_adjacency(0, 0, 1)
        quantise_adjacency(0, 1, 1)

        def stage1_block(b):
            for n in range(b * BLOCK, (b + 1) * BLOCK):
                stage1_bank(n)

        def quantise_block(b):
            quantise_stage1(b // PASSES, b % PASSES)

        later_transposes = [
            lambda: transpose_nodes(1, 1),
            lambda: transpose_adjacency(0, 0),
            lambda: transpose_adjacency(1, 0),
            lambda: transpose_adjacency(0, 1),
            lambda: transpose_adjacency(1, 1),
        ]
        later_quantises = [
            lambda: quantise_nodes(1, 0),
            lambda: quantise_nodes(1, 1),
            lambda: quantise_adjacency(1, 0, 0),
            lambda: quantise_adjacency(1, 1, 0),
            lambda: quantise_adjacency(1, 0, 1),
            lambda: quantise_adjacency(1, 1, 1),
        ]

        pending = []
        for r in range(ROUNDS):
            first = r * BLOCK
            ahead = r + LEAD_BLOCKS
            stage2_bank(first + 0)
            while pending:
                pending.pop()()
            if ahead < ROUNDS:
                stage1_bank(ahead * BLOCK + 0)
            stage2_bank(first + 1)
            if ahead < ROUNDS:
                stage1_bank(ahead * BLOCK + 1)
            if ahead < ROUNDS:
                stage1_bank(ahead * BLOCK + 2)
            if ahead < ROUNDS:
                stage1_bank(ahead * BLOCK + 3)
            stage2_bank(first + 2)
            if r < len(later_quantises):
                later_quantises[r]()
            if r == 5:
                degree_in_reciprocals()
            if r < len(later_transposes):
                later_transposes[r]()
            stage2_bank(first + 3)
            if ahead < ROUNDS:
                quantise_block(ahead)
            if r in (2, 4):
                pending.append(degree_in(2 + r))
